import numpy as np
import ml_dtypes


def mxq(x, axis, fmt="e4m3"):
    dtype, down = {"e4m3": (ml_dtypes.float8_e4m3fn, 7), "e5m2": (ml_dtypes.float8_e5m2, 14)}[fmt]
    v = np.moveaxis(np.asarray(x, np.float32).astype(ml_dtypes.bfloat16).astype(np.float64), axis, -1)
    blocks = v.reshape(v.shape[:-1] + (-1, 32))
    amax = np.abs(blocks).max(-1, keepdims=True)
    byte = np.maximum(np.where(amax > 0, np.frexp(amax)[1] - 1 + 127, 0) - down, 1)
    scale = np.exp2(byte - 127.0)
    codes = (blocks / scale).astype(np.float32).astype(dtype).astype(np.float64)
    return np.moveaxis((codes * scale).reshape(v.shape), -1, axis)


WIDE = False


def mx_kscale(k):
    if not WIDE:
        return np.ones(k)
    levels = np.array([10, -10, 5, -5, 0])
    if k % 512:
        return np.exp2(np.random.permutation(np.resize(levels, k // 32))).repeat(32)
    a = np.empty((k // 512, 16))
    for p in range(k // 512):
        a[p, :8] = np.random.permutation(np.resize(levels, 8))
        for g in range(8):
            far = levels[np.abs(levels - a[p, g]) >= 10]
            a[p, g + 8] = far[np.random.randint(len(far))]
    return np.exp2(a.ravel()).repeat(32)


BF16 = ml_dtypes.bfloat16


def bf(x):
    return np.asarray(x, np.float32).astype(BF16)


def f64(x):
    return np.asarray(x).astype(np.float64)


B, C, H, W, M, O = 2, 8192, 16, 16, 512, 512
N = B * H * W
L2_EPS = 1e-12
BN_EPS = 1e-5


def l2_normalize(x, axis):
    n = np.sqrt(np.sum(x * x, axis=axis, keepdims=True))
    return x / np.maximum(n, L2_EPS)


def setup_inputs():
    s = mx_kscale(C)
    cm = (np.random.standard_normal((N, C)) * 5.0 + np.random.standard_normal((1, C)) * 1.5) / np.sqrt(C)
    w = np.random.standard_normal((O, 2 * C)) * 0.1 / np.sqrt(2 * C)
    w[:, C:] = w[:, C:] / s
    return {"query": bf(np.random.standard_normal((B, C, H, W))), "concat_memory": bf(cm * s), "conv_w": bf(w),
            "bn_gamma": bf(1.0 + 0.1 * np.random.standard_normal(O)), "bn_beta": bf(0.2 * np.random.standard_normal(O))}


def reference(query, concat_memory, conv_w, bn_gamma, bn_beta):
    q_flat = l2_normalize(f64(query), 1).transpose(0, 2, 3, 1).reshape(N, C)
    upd = np.concatenate([q_flat, f64(concat_memory)], axis=1)
    y = mxq(upd, 1, "e4m3") @ mxq(f64(conv_w), 1, "e4m3").T
    y = y.reshape(B, H, W, O).transpose(0, 3, 1, 2)
    mean = np.mean(y, axis=(0, 2, 3), keepdims=True)
    var = np.mean((y - mean) ** 2, axis=(0, 2, 3), keepdims=True)
    y = (y - mean) / np.sqrt(var + BN_EPS)
    y = y * f64(bn_gamma)[None, :, None, None] + f64(bn_beta)[None, :, None, None]
    return np.maximum(y, 0.0)

@@ -1,0 +1,303 @@
+from contextlib import ExitStack
+
+import concourse.mybir as mybir
+from concourse.masks import make_identity
+
+F32 = mybir.dt.float32
+BF16 = mybir.dt.bfloat16
+U32 = mybir.dt.uint32
+U8 = mybir.dt.uint8
+FP8X4 = mybir.dt.float8_e4m3fn_x4
+ACT = mybir.ActivationFunctionType
+ALU = mybir.AluOpType
+AXIS = mybir.AxisListType
+
+P = 128
+BATCH = 2
+CHANNELS = 8192
+PIXELS = 256
+ROWS = BATCH * PIXELS
+OUT_CH = 512
+TILES = OUT_CH // P
+K_PASS = 4 * P
+HALF_PASSES = CHANNELS // K_PASS
+CHUNK_PASSES = 2
+K_CHUNK = CHUNK_PASSES * K_PASS
+PLANES = CHANNELS // P
+BANK_PLANES = 4
+BATCH_BANKS = PLANES // BANK_PLANES
+SLAB_PLANES = 8
+FAST_BANKS = 4
+FAST_PASSES = BATCH_BANKS // FAST_BANKS
+SLOW_BANKS = 2
+SLOW_PASSES = BATCH_BANKS // SLOW_BANKS
+SLICES_PER_PASS = HALF_PASSES // SLOW_PASSES
+RUN = 4
+AHEAD = 2
+LAG = 2
+L2_EPS = 1e-12
+BN_EPS = 1e-5
+
+FLOPS = 2 * ROWS * OUT_CH * 2 * CHANNELS
+
+
+def tile_memory_sup_pb_k_kernel(tc, query, concat_memory, conv_w, bn_gamma, bn_beta, out):
+    nc = tc.nc
+    with ExitStack() as ctx:
+        const = ctx.enter_context(tc.tile_pool(name="const", bufs=1))
+        rows_pool = ctx.enter_context(tc.tile_pool(name="rows", bufs=AHEAD + 1))
+        work = ctx.enter_context(tc.tile_pool(name="work", bufs=LAG + 1))
+        scratch = ctx.enter_context(tc.tile_pool(name="scratch", bufs=4))
+        acc_pool = ctx.enter_context(tc.psum_pool(name="acc", bufs=1))
+        bank_pool = ctx.enter_context(tc.psum_pool(name="bank", bufs=4))
+
+        gb_rows = const.tile([P, P], BF16)
+        nc.vector.memset(gb_rows[:], 0.0)
+        nc.scalar.dma_start(out=gb_rows[0:TILES, :], in_=bn_gamma.rearrange("(t p) -> t p", p=P))
+        nc.scalar.dma_start(out=gb_rows[TILES : 2 * TILES, :], in_=bn_beta.rearrange("(t p) -> t p", p=P))
+        gamma_beta = const.tile([P, 2 * TILES], F32)
+        ones = const.tile([P, P], F32)
+        nc.vector.memset(ones[:], 1.0)
+        warm = const.tile([P, 1], F32)
+        nc.scalar.sqrt(out=warm[:], in_=ones[:, 0:1])
+        ident = const.tile([P, P], F32)
+        make_identity(nc, ident[:])
+
+        q_sb = const.tile([P, BATCH, PLANES, PIXELS], BF16)
+        sum_sq = const.tile([P, BATCH, 2, BATCH_BANKS], F32)
+        inv_norm = const.tile([P, BATCH, PIXELS], F32)
+        q_codes = const.tile([P, HALF_PASSES, ROWS], U32, align_bytes=64)
+        q_scales = const.tile([P, HALF_PASSES, ROWS], U8, align_bytes=64)
+        acc = [acc_pool.tile([P, ROWS], F32, name="acc%d" % t) for t in range(TILES)]
+
+        def load_slab(slab):
+            b, first = divmod(slab * SLAB_PLANES, PLANES)
+            nc.sync.dma_start(
+                out=q_sb[:, b, first : first + SLAB_PLANES, :].rearrange("p (s e) n -> p s (e n)", e=4),
+                in_=query[b, first * P : (first + SLAB_PLANES) * P].rearrange("(s p e) h w -> p s (e h w)", p=P, e=4),
+            )
+
+        passes = [("memory", g) for g in range(HALF_PASSES)] + [("query", g) for g in range(HALF_PASSES)]
+        chunk_rows = {}
+
+        def load_chunk(c):
+            kind, g = passes[c * CHUNK_PASSES]
+            first = g * K_PASS
+            w_first = first + (CHANNELS if kind == "memory" else 0)
+            w_rows = rows_pool.tile([P, TILES, K_CHUNK], BF16, tag="w_rows")
+            nc.sync.dma_start(
+                out=w_rows[:], in_=conv_w[:, w_first : w_first + K_CHUNK].rearrange("(t p) k -> p t k", p=P)
+            )
+            m_rows = None
+            if kind == "memory":
+                m_rows = rows_pool.tile([P, TILES, K_CHUNK], BF16, tag="m_rows")
+                nc.sync.dma_start(
+                    out=m_rows[:], in_=concat_memory[:, first : first + K_CHUNK].rearrange("(t p) k -> p t k", p=P)
+                )
+            chunk_rows[c] = (w_rows, m_rows)
+
+        def banks_squared(i):
+            if i < FAST_PASSES:
+                return range(FAST_BANKS * i, FAST_BANKS * (i + 1))
+            if i < FAST_PASSES + SLOW_PASSES:
+                first = BATCH_BANKS + SLOW_BANKS * (i - FAST_PASSES)
+                return range(first, first + SLOW_BANKS)
+            return range(0)
+
+        def load_for_chunk(c):
+            if c * CHUNK_PASSES >= len(passes):
+                return
+            banks = [k for i in range(c * CHUNK_PASSES, (c + 1) * CHUNK_PASSES) for k in banks_squared(i)]
+            slabs = sorted(set(k * BANK_PLANES // SLAB_PLANES for k in banks))
+            for slab in slabs[:1]:
+                load_slab(slab)
+            load_chunk(c)
+            for slab in slabs[1:]:
+                load_slab(slab)
+
+        def transpose_rows(rows, local, pair, grouped_words, copy):
+            bank = bank_pool.tile([P, 4, P], F32, tag="bank")
+            for j in range(4):
+                t, u = 2 * pair + j // 2, j % 2
+                first = 2 * local * P
+                nc.tensor.transpose(
+                    bank[:, j, :], rows[:, t, :].bitcast(F32)[:, first + u : first + 2 * P : 2], ident[:]
+                )
+            copy(
+                out=grouped_words[:, 4 * P * pair : 4 * P * (pair + 1)].rearrange("p (t r u) -> p t r u", t=2, u=2),
+                in_=bank[:].rearrange("p (t u) r -> p t r u", u=2),
+            )
+
+        def square_bank(k):
+            b, first = divmod(k * BANK_PLANES, PLANES)
+            bank = bank_pool.tile([P, 4, P], F32, tag="bank")
+            for j in range(BANK_PLANES):
+                nc.tensor.transpose(bank[:, j, :], q_sb[:, b, first + j, :].bitcast(F32), ident[:])
+            by_parity = bank[:].bitcast(BF16).rearrange("p j (c h) -> p h j c", h=2)
+            for h in range(2):
+                squares = scratch.tile([P, 4, P], BF16, tag="squares")
+                nc.scalar.activation(
+                    out=squares[:],
+                    in_=by_parity[:, h],
+                    func=ACT.Square,
+                    accum_out=sum_sq[:, b, h, k % BATCH_BANKS : k % BATCH_BANKS + 1],
+                )
+
+        repeated_of = {}
+
+        def pixel_scales_start(b):
+            total = scratch.tile([P, 2], F32, tag="total")
+            nc.vector.tensor_reduce(out=total[:], in_=sum_sq[:, b], axis=AXIS.X, op=ALU.add)
+            floored = scratch.tile([P, 2], F32, tag="floored")
+            nc.vector.tensor_scalar_max(out=floored[:], in0=total[:], scalar1=L2_EPS * L2_EPS)
+            norm = scratch.tile([P, 2], F32, tag="norm")
+            nc.scalar.sqrt(out=norm[:], in_=floored[:])
+            inv = scratch.tile([P, 2], F32, tag="inv")
+            nc.vector.reciprocal(out=inv[:], in_=norm[:])
+            repeated = scratch.tile([P, 2, P], F32, tag="repeated")
+            for h in range(2):
+                nc.vector.tensor_scalar_mul(out=repeated[:, h, :], in0=ones[:], scalar1=inv[:, h : h + 1])
+            repeated_of[b] = repeated
+
+        def pixel_scales_finish(b):
+            bank = bank_pool.tile([P, 4, P], F32, tag="bank")
+            for h in range(2):
+                nc.tensor.transpose(bank[:, h, :], repeated_of[b][:, h, :], ident[:])
+            nc.vector.tensor_copy(
+                out=inv_norm[:, b, :].rearrange("p (w h) -> p w h", h=2),
+                in_=bank[:, 0:2, :].rearrange("p h w -> p w h"),
+            )
+
+        def transpose_gamma_beta():
+            gb_f32 = const.tile([P, P], F32)
+            nc.vector.tensor_copy(out=gb_f32[:], in_=gb_rows[:])
+            bank = bank_pool.tile([P, 4, P], F32, tag="bank")
+            nc.tensor.transpose(bank[:, 0, :], gb_f32[:], ident[:])
+            nc.vector.tensor_copy(out=gamma_beta[:], in_=bank[:, 0, 0 : 2 * TILES])
+
+        def normalise(b, first, count):
+            q_flat = work.tile([P, count, PIXELS, 4], BF16, tag="q_flat", align_bytes=64)
+            for k in range(count):
+                g = first + k
+                nc.vector.tensor_tensor(
+                    out=q_flat[:, k].rearrange("p (c i) t -> p c t i", i=RUN),
+                    in0=q_sb[:, b, 4 * g : 4 * g + 4, :].rearrange("p t (c i) -> p c t i", i=RUN),
+                    in1=inv_norm[:, b, :]
+                    .rearrange("p (c i) -> p c i", i=RUN)
+                    .unsqueeze(2)
+                    .to_broadcast([P, PIXELS // RUN, 4, RUN]),
+                    op=ALU.mult,
+                )
+            return [(b, first + k, q_flat[:, k].rearrange("p n t -> p (n t)")) for k in range(count)]
+
+        def quantise_slices(slices):
+            for b, g, q_flat in slices:
+                pixels = slice(b * PIXELS, (b + 1) * PIXELS)
+                nc.vector.quantize_mx(out=q_codes[:, g, pixels].bitcast(FP8X4), scales=q_scales[:, g, pixels], in_=q_flat)
+
+        grouped_of = {}
+        operands_of = {}
+
+        def prepare(i):
+            kind, g = passes[i]
+            c, local = divmod(i, CHUNK_PASSES)
+            if local == 0:
+                load_for_chunk(c + AHEAD)
+            w_rows, m_rows = chunk_rows[c]
+            copy = nc.vector.tensor_copy if i < FAST_PASSES else nc.scalar.copy
+            grouped = work.tile([P, 4 * (OUT_CH + ROWS)], BF16, tag="grouped", align_bytes=64)
+            words = grouped[:].bitcast(F32)
+            to_copy = [(w_rows, pair, words[:, 0 : 2 * OUT_CH]) for pair in range(TILES // 2)]
+            if kind == "memory":
+                to_copy.extend([(m_rows, pair, words[:, 2 * OUT_CH : 2 * (OUT_CH + ROWS)]) for pair in range(TILES // 2)])
+            to_square = list(banks_squared(i))
+            due = [b for b in range(BATCH) if i == (FAST_PASSES, FAST_PASSES + SLOW_PASSES)[b]]
+            for b in due:
+                pixel_scales_start(b)
+            for k in range(len(to_copy)):
+                if k < len(to_square):
+                    square_bank(to_square[k])
+                rows, pair, half = to_copy[k]
+                transpose_rows(rows, local, pair, half, copy)
+            for b in due:
+                pixel_scales_finish(b)
+            if i == FAST_PASSES + SLOW_PASSES:
+                transpose_gamma_beta()
+            grouped_of[i] = grouped
+            if FAST_PASSES <= i < FAST_PASSES + SLOW_PASSES:
+                return normalise(0, SLICES_PER_PASS * (i - FAST_PASSES), SLICES_PER_PASS)
+            if kind == "query":
+                return normalise(1, g, 1)
+            return []
+
+        def quantise(i):
+            width = OUT_CH + (ROWS if passes[i][0] == "memory" else 0)
+            codes = work.tile([P, OUT_CH + ROWS], U32, tag="codes", align_bytes=64)
+            scales = work.tile([P, OUT_CH + ROWS], U8, tag="scales", align_bytes=64)
+            nc.vector.quantize_mx(
+                out=codes[:, 0:width].bitcast(FP8X4), scales=scales[:, 0:width], in_=grouped_of[i][:, 0 : 4 * width]
+            )
+            operands_of[i] = (codes, scales)
+
+        def multiply(i, t):
+            kind, g = passes[i]
+            codes, scales = operands_of[i]
+            if kind == "memory":
+                upd_codes, upd_scales = codes[:, OUT_CH : OUT_CH + ROWS], scales[:, OUT_CH : OUT_CH + ROWS]
+            else:
+                upd_codes, upd_scales = q_codes[:, g, :], q_scales[:, g, :]
+            nc.tensor.matmul_mx(
+                out=acc[t][:],
+                lhsT=codes[:, t * P : (t + 1) * P].bitcast(FP8X4),
+                lhsT_scale=scales[:, t * P : (t + 1) * P],
+                rhs=upd_codes.bitcast(FP8X4),
+                rhs_scale=upd_scales,
+                start=(i == 0),
+                stop=(i == len(passes) - 1),
+            )
+
+        for c in range(AHEAD):
+            load_for_chunk(c)
+
+        with tc.manual_schedule():
+            for i in range(len(passes)):
+                slices = prepare(i)
+                if i >= 1:
+                    quantise(i - 1)
+                quantise_slices(slices)
+                if i >= LAG:
+                    for t in range(TILES):
+                        multiply(i - LAG, t)
+            quantise(len(passes) - 1)
+            for t in range(TILES):
+                for i in range(len(passes) - LAG, len(passes)):
+                    multiply(i, t)
+
+        stats = const.tile([P, TILES, 6], F32)
+        mean_var = const.tile([P, TILES, 2], F32)
+        for t in range(TILES):
+            nc.vector.bn_stats(out=stats[:, t, :], in_=acc[t][:])
+            nc.vector.bn_aggr(out=mean_var[:, t, :], in_=stats[:, t, :])
+        var_eps = const.tile([P, TILES], F32)
+        nc.vector.tensor_scalar_add(out=var_eps[:], in0=mean_var[:, :, 1], scalar1=BN_EPS)
+        std = const.tile([P, TILES], F32)
+        nc.scalar.sqrt(out=std[:], in_=var_eps[:])
+        inv_std = const.tile([P, TILES], F32)
+        nc.vector.reciprocal(out=inv_std[:], in_=std[:])
+        gain = const.tile([P, TILES], F32)
+        nc.vector.tensor_tensor(out=gain[:], in0=gamma_beta[:, 0:TILES], in1=inv_std[:], op=ALU.mult)
+        mean_gain = const.tile([P, TILES], F32)
+        nc.vector.tensor_tensor(out=mean_gain[:], in0=mean_var[:, :, 0], in1=gain[:], op=ALU.mult)
+        shift = const.tile([P, TILES], F32)
+        nc.vector.tensor_tensor(out=shift[:], in0=gamma_beta[:, TILES : 2 * TILES], in1=mean_gain[:], op=ALU.subtract)
+        out_tiles = out.rearrange("b (t p) h w -> t p b (h w)", p=P)
+        for t in range(TILES):
+            result = scratch.tile([P, BATCH, PIXELS], F32, tag="result")
+            nc.scalar.activation(
+                out=result[:].rearrange("p b n -> p (b n)"),
+                in_=acc[t][:],
+                func=ACT.Relu,
+                scale=gain[:, t : t + 1],
+                bias=shift[:, t : t + 1],
+            )
+            nc.sync.dma_start(out=out_tiles[t], in_=result[:])

@@ -27,12 +27,16 @@ PLANES = CHANNELS // P
 BANK_PLANES = 4
 BATCH_BANKS = PLANES // BANK_PLANES
 SLAB_PLANES = 8
-FAST_BANKS = 4
-FAST_PASSES = BATCH_BANKS // FAST_BANKS
-SLOW_BANKS = 2
-SLOW_PASSES = BATCH_BANKS // SLOW_BANKS
-SLICES_PER_PASS = HALF_PASSES // SLOW_PASSES
+BATCH_SLABS = PLANES // SLAB_PLANES
+GRAM_PASSES = 3
+GRAM_SLABS = -(-BATCH_SLABS // GRAM_PASSES)
+SQUARE_BANKS = 2
+SQUARE_PASSES = BATCH_BANKS // SQUARE_BANKS
+SQUARE_END = GRAM_PASSES + SQUARE_PASSES
 RUN = 4
+TRANSPOSE_BANKS = 4
+SHARED_SLICES = 1
+FREE_SLICES = 2
 AHEAD = 2
 LAG = 2
 L2_EPS = 1e-12
@@ -49,7 +53,7 @@ def tile_memory_sup_pb_k_kernel(tc, query, concat_memory, conv_w, bn_gamma, bn_b
         work = ctx.enter_context(tc.tile_pool(name="work", bufs=LAG + 1))
         scratch = ctx.enter_context(tc.tile_pool(name="scratch", bufs=4))
         acc_pool = ctx.enter_context(tc.psum_pool(name="acc", bufs=1))
-        bank_pool = ctx.enter_context(tc.psum_pool(name="bank", bufs=4))
+        bank_pool = ctx.enter_context(tc.psum_pool(name="bank", bufs=1))
 
         gb_rows = const.tile([P, P], BF16)
         nc.vector.memset(gb_rows[:], 0.0)
@@ -64,7 +68,7 @@ def tile_memory_sup_pb_k_kernel(tc, query, concat_memory, conv_w, bn_gamma, bn_b
         make_identity(nc, ident[:])
 
         q_sb = const.tile([P, BATCH, PLANES, PIXELS], BF16)
-        sum_sq = const.tile([P, BATCH, 2, BATCH_BANKS], F32)
+        sum_sq = const.tile([P, 2, BATCH_BANKS], F32)
         inv_norm = const.tile([P, BATCH, PIXELS], F32)
         q_codes = const.tile([P, HALF_PASSES, ROWS], U32, align_bytes=64)
         q_scales = const.tile([P, HALF_PASSES, ROWS], U8, align_bytes=64)
@@ -80,43 +84,54 @@ def tile_memory_sup_pb_k_kernel(tc, query, concat_memory, conv_w, bn_gamma, bn_b
         passes = [("memory", g) for g in range(HALF_PASSES)] + [("query", g) for g in range(HALF_PASSES)]
         chunk_rows = {}
 
-        def load_chunk(c):
-            kind, g = passes[c * CHUNK_PASSES]
+        def load_rows(c, kind):
+            half, g = passes[c * CHUNK_PASSES]
             first = g * K_PASS
-            w_first = first + (CHANNELS if kind == "memory" else 0)
-            w_rows = rows_pool.tile([P, TILES, K_CHUNK], BF16, tag="w_rows")
+            if kind == "w":
+                source, column = conv_w, first + (CHANNELS if half == "memory" else 0)
+            else:
+                source, column = concat_memory, first
+            rows = rows_pool.tile([P, TILES, K_CHUNK], BF16, tag="%s_rows" % kind)
             nc.sync.dma_start(
-                out=w_rows[:], in_=conv_w[:, w_first : w_first + K_CHUNK].rearrange("(t p) k -> p t k", p=P)
+                out=rows[:], in_=source[:, column : column + K_CHUNK].rearrange("(t p) k -> p t k", p=P)
             )
-            m_rows = None
-            if kind == "memory":
-                m_rows = rows_pool.tile([P, TILES, K_CHUNK], BF16, tag="m_rows")
-                nc.sync.dma_start(
-                    out=m_rows[:], in_=concat_memory[:, first : first + K_CHUNK].rearrange("(t p) k -> p t k", p=P)
-                )
-            chunk_rows[c] = (w_rows, m_rows)
+            chunk_rows[c, kind] = rows
+
+        banks = {"next": 0, "count": TRANSPOSE_BANKS - 1}
+
+        def next_bank():
+            k = banks["next"]
+            banks["next"] = (k + 1) % banks["count"]
+            return bank_pool.tile([P, 4, P], F32, tag="bank%d" % k, name="bank%d" % k)
+
+        def slabs_multiplied(i):
+            if i < GRAM_PASSES:
+                return range(GRAM_SLABS * i, min(GRAM_SLABS * (i + 1), BATCH_SLABS))
+            return range(0)
 
         def banks_squared(i):
-            if i < FAST_PASSES:
-                return range(FAST_BANKS * i, FAST_BANKS * (i + 1))
-            if i < FAST_PASSES + SLOW_PASSES:
-                first = BATCH_BANKS + SLOW_BANKS * (i - FAST_PASSES)
-                return range(first, first + SLOW_BANKS)
+            if GRAM_PASSES <= i < SQUARE_END:
+                return range(SQUARE_BANKS * (i - GRAM_PASSES), SQUARE_BANKS * (i - GRAM_PASSES + 1))
             return range(0)
 
         def load_for_chunk(c):
             if c * CHUNK_PASSES >= len(passes):
                 return
-            banks = [k for i in range(c * CHUNK_PASSES, (c + 1) * CHUNK_PASSES) for k in banks_squared(i)]
-            slabs = sorted(set(k * BANK_PLANES // SLAB_PLANES for k in banks))
+            chunk = range(c * CHUNK_PASSES, (c + 1) * CHUNK_PASSES)
+            slabs = [s for i in chunk for s in slabs_multiplied(i)]
+            slabs.extend(sorted(set(BATCH_SLABS + k * BANK_PLANES // SLAB_PLANES for i in chunk for k in banks_squared(i))))
             for slab in slabs[:1]:
                 load_slab(slab)
-            load_chunk(c)
-            for slab in slabs[1:]:
+            load_rows(c, "w")
+            for slab in slabs[1:2]:
+                load_slab(slab)
+            if passes[c * CHUNK_PASSES][0] == "memory":
+                load_rows(c, "m")
+            for slab in slabs[2:]:
                 load_slab(slab)
 
         def transpose_rows(rows, local, pair, grouped_words, copy):
-            bank = bank_pool.tile([P, 4, P], F32, tag="bank")
+            bank = next_bank()
             for j in range(4):
                 t, u = 2 * pair + j // 2, j % 2
                 first = 2 * local * P
@@ -129,10 +144,9 @@ def tile_memory_sup_pb_k_kernel(tc, query, concat_memory, conv_w, bn_gamma, bn_b
             )
 
         def square_bank(k):
-            b, first = divmod(k * BANK_PLANES, PLANES)
-            bank = bank_pool.tile([P, 4, P], F32, tag="bank")
+            bank = next_bank()
             for j in range(BANK_PLANES):
-                nc.tensor.transpose(bank[:, j, :], q_sb[:, b, first + j, :].bitcast(F32), ident[:])
+                nc.tensor.transpose(bank[:, j, :], q_sb[:, 1, k * BANK_PLANES + j, :].bitcast(F32), ident[:])
             by_parity = bank[:].bitcast(BF16).rearrange("p j (c h) -> p h j c", h=2)
             for h in range(2):
                 squares = scratch.tile([P, 4, P], BF16, tag="squares")
@@ -140,14 +154,54 @@ def tile_memory_sup_pb_k_kernel(tc, query, concat_memory, conv_w, bn_gamma, bn_b
                     out=squares[:],
                     in_=by_parity[:, h],
                     func=ACT.Square,
-                    accum_out=sum_sq[:, b, h, k % BATCH_BANKS : k % BATCH_BANKS + 1],
+                    accum_out=sum_sq[:, h, k : k + 1],
                 )
 
-        repeated_of = {}
+        gram = bank_pool.tile([P, 2, P], F32, tag="bank%d" % (TRANSPOSE_BANKS - 1), name="gram")
 
-        def pixel_scales_start(b):
+        def multiply_slab(slab):
+            for plane in range(slab * SLAB_PLANES, (slab + 1) * SLAB_PLANES):
+                for h in range(2):
+                    half = q_sb[:, 0, plane, h * P : (h + 1) * P]
+                    nc.tensor.matmul(
+                        gram[:, h, :],
+                        lhsT=half,
+                        rhs=half,
+                        start=(plane == 0 and h == 0),
+                        stop=(plane == PLANES - 1 and h == 1),
+                    )
+
+        scales_of = {}
+
+        def batch_0_scales_start():
+            diagonal = scratch.tile([P, 2, P], F32, tag="diagonal")
+            nc.vector.tensor_tensor(
+                out=diagonal[:], in0=gram[:], in1=ident[:].unsqueeze(1).to_broadcast([P, 2, P]), op=ALU.mult
+            )
+            banks["count"] = TRANSPOSE_BANKS
+            scales_of["diagonal"] = diagonal
+
+        def batch_0_scales_spread():
+            bank = next_bank()
+            nc.tensor.matmul(
+                bank[:, 0:2, :].rearrange("p h r -> p (h r)"),
+                lhsT=ones[:],
+                rhs=scales_of["diagonal"][:].rearrange("p h r -> p (h r)"),
+                start=True,
+                stop=True,
+            )
+            norm = scratch.tile([P, PIXELS], F32, tag="norms")
+            nc.scalar.sqrt(out=norm[:], in_=bank[:, 0:2, :].rearrange("p h r -> p (h r)"))
+            scales_of["norm"] = norm
+
+        def batch_0_scales_finish():
+            floored = scratch.tile([P, PIXELS], F32, tag="norms")
+            nc.vector.tensor_scalar_max(out=floored[:], in0=scales_of["norm"][:], scalar1=L2_EPS)
+            nc.vector.reciprocal(out=inv_norm[:, 0, :], in_=floored[:])
+
+        def batch_1_scales_start():
             total = scratch.tile([P, 2], F32, tag="total")
-            nc.vector.tensor_reduce(out=total[:], in_=sum_sq[:, b], axis=AXIS.X, op=ALU.add)
+            nc.vector.tensor_reduce(out=total[:], in_=sum_sq[:], axis=AXIS.X, op=ALU.add)
             floored = scratch.tile([P, 2], F32, tag="floored")
             nc.vector.tensor_scalar_max(out=floored[:], in0=total[:], scalar1=L2_EPS * L2_EPS)
             norm = scratch.tile([P, 2], F32, tag="norm")
@@ -157,30 +211,32 @@ def tile_memory_sup_pb_k_kernel(tc, query, concat_memory, conv_w, bn_gamma, bn_b
             repeated = scratch.tile([P, 2, P], F32, tag="repeated")
             for h in range(2):
                 nc.vector.tensor_scalar_mul(out=repeated[:, h, :], in0=ones[:], scalar1=inv[:, h : h + 1])
-            repeated_of[b] = repeated
+            scales_of["repeated"] = repeated
 
-        def pixel_scales_finish(b):
-            bank = bank_pool.tile([P, 4, P], F32, tag="bank")
+        def batch_1_scales_finish():
+            bank = next_bank()
             for h in range(2):
-                nc.tensor.transpose(bank[:, h, :], repeated_of[b][:, h, :], ident[:])
+                nc.tensor.transpose(bank[:, h, :], scales_of["repeated"][:, h, :], ident[:])
             nc.vector.tensor_copy(
-                out=inv_norm[:, b, :].rearrange("p (w h) -> p w h", h=2),
+                out=inv_norm[:, 1, :].rearrange("p (w h) -> p w h", h=2),
                 in_=bank[:, 0:2, :].rearrange("p h w -> p w h"),
             )
 
         def transpose_gamma_beta():
             gb_f32 = const.tile([P, P], F32)
             nc.vector.tensor_copy(out=gb_f32[:], in_=gb_rows[:])
-            bank = bank_pool.tile([P, 4, P], F32, tag="bank")
+            bank = next_bank()
             nc.tensor.transpose(bank[:, 0, :], gb_f32[:], ident[:])
             nc.vector.tensor_copy(out=gamma_beta[:], in_=bank[:, 0, 0 : 2 * TILES])
 
-        def normalise(b, first, count):
-            q_flat = work.tile([P, count, PIXELS, 4], BF16, tag="q_flat", align_bytes=64)
-            for k in range(count):
-                g = first + k
+        slices_left = [(b, g) for b in range(BATCH) for g in range(HALF_PASSES)]
+
+        def normalise(slices):
+            made = []
+            for b, g in slices:
+                q_flat = work.tile([P, PIXELS, 4], BF16, tag="q_flat", align_bytes=64)
                 nc.vector.tensor_tensor(
-                    out=q_flat[:, k].rearrange("p (c i) t -> p c t i", i=RUN),
+                    out=q_flat[:].rearrange("p (c i) t -> p c t i", i=RUN),
                     in0=q_sb[:, b, 4 * g : 4 * g + 4, :].rearrange("p t (c i) -> p c t i", i=RUN),
                     in1=inv_norm[:, b, :]
                     .rearrange("p (c i) -> p c i", i=RUN)
@@ -188,7 +244,8 @@ def tile_memory_sup_pb_k_kernel(tc, query, concat_memory, conv_w, bn_gamma, bn_b
                     .to_broadcast([P, PIXELS // RUN, 4, RUN]),
                     op=ALU.mult,
                 )
-            return [(b, first + k, q_flat[:, k].rearrange("p n t -> p (n t)")) for k in range(count)]
+                made.append((b, g, q_flat[:].rearrange("p n t -> p (n t)")))
+            return made
 
         def quantise_slices(slices):
             for b, g, q_flat in slices:
@@ -203,32 +260,44 @@ def tile_memory_sup_pb_k_kernel(tc, query, concat_memory, conv_w, bn_gamma, bn_b
             c, local = divmod(i, CHUNK_PASSES)
             if local == 0:
                 load_for_chunk(c + AHEAD)
-            w_rows, m_rows = chunk_rows[c]
-            copy = nc.vector.tensor_copy if i < FAST_PASSES else nc.scalar.copy
+            w_rows = chunk_rows[c, "w"]
             grouped = work.tile([P, 4 * (OUT_CH + ROWS)], BF16, tag="grouped", align_bytes=64)
             words = grouped[:].bitcast(F32)
             to_copy = [(w_rows, pair, words[:, 0 : 2 * OUT_CH]) for pair in range(TILES // 2)]
             if kind == "memory":
+                m_rows = chunk_rows[c, "m"]
                 to_copy.extend([(m_rows, pair, words[:, 2 * OUT_CH : 2 * (OUT_CH + ROWS)]) for pair in range(TILES // 2)])
+            to_multiply = list(slabs_multiplied(i))
             to_square = list(banks_squared(i))
-            due = [b for b in range(BATCH) if i == (FAST_PASSES, FAST_PASSES + SLOW_PASSES)[b]]
-            for b in due:
-                pixel_scales_start(b)
+            if i == SQUARE_END:
+                batch_1_scales_start()
             for k in range(len(to_copy)):
+                if k < len(to_multiply):
+                    multiply_slab(to_multiply[k])
                 if k < len(to_square):
                     square_bank(to_square[k])
                 rows, pair, half = to_copy[k]
-                transpose_rows(rows, local, pair, half, copy)
-            for b in due:
-                pixel_scales_finish(b)
-            if i == FAST_PASSES + SLOW_PASSES:
+                on_vector = i < SQUARE_END and rows is w_rows
+                transpose_rows(rows, local, pair, half, nc.vector.tensor_copy if on_vector else nc.scalar.copy)
+            if i == GRAM_PASSES - 1:
+                batch_0_scales_start()
+            if i == GRAM_PASSES:
+                batch_0_scales_finish()
+            if i == SQUARE_END:
+                batch_1_scales_finish()
                 transpose_gamma_beta()
             grouped_of[i] = grouped
-            if FAST_PASSES <= i < FAST_PASSES + SLOW_PASSES:
-                return normalise(0, SLICES_PER_PASS * (i - FAST_PASSES), SLICES_PER_PASS)
-            if kind == "query":
-                return normalise(1, g, 1)
-            return []
+            if i < GRAM_PASSES:
+                count = 0
+            elif i < SQUARE_END:
+                count = SHARED_SLICES
+            elif kind == "memory":
+                count = FREE_SLICES
+            else:
+                count = 1
+            slices = slices_left[:count]
+            slices_left[:] = slices_left[count:]
+            return normalise(slices)
 
         def quantise(i):
             width = OUT_CH + (ROWS if passes[i][0] == "memory" else 0)
@@ -268,6 +337,8 @@ def tile_memory_sup_pb_k_kernel(tc, query, concat_memory, conv_w, bn_gamma, bn_b
                 if i >= LAG:
                     for t in range(TILES):
                         multiply(i - LAG, t)
+                if i == GRAM_PASSES - 1:
+                    batch_0_scales_spread()
             quantise(len(passes) - 1)
             for t in range(TILES):
                 for i in range(len(passes) - LAG, len(passes)):

@@ -50,8 +50,9 @@ def tile_memory_sup_pb_k_kernel(tc, query, concat_memory, conv_w, bn_gamma, bn_b
     with ExitStack() as ctx:
         const = ctx.enter_context(tc.tile_pool(name="const", bufs=1))
         rows_pool = ctx.enter_context(tc.tile_pool(name="rows", bufs=AHEAD + 1))
+        ordered_pool = ctx.enter_context(tc.tile_pool(name="ordered", bufs=2))
         work = ctx.enter_context(tc.tile_pool(name="work", bufs=LAG + 1))
-        scratch = ctx.enter_context(tc.tile_pool(name="scratch", bufs=4))
+        scratch = ctx.enter_context(tc.tile_pool(name="scratch", bufs=2))
         acc_pool = ctx.enter_context(tc.psum_pool(name="acc", bufs=1))
         bank_pool = ctx.enter_context(tc.psum_pool(name="bank", bufs=1))
 
@@ -84,18 +85,19 @@ def tile_memory_sup_pb_k_kernel(tc, query, concat_memory, conv_w, bn_gamma, bn_b
         passes = [("memory", g) for g in range(HALF_PASSES)] + [("query", g) for g in range(HALF_PASSES)]
         chunk_rows = {}
 
-        def load_rows(c, kind):
+        def load_rows(c, kind, first, count):
             half, g = passes[c * CHUNK_PASSES]
-            first = g * K_PASS
+            column = (g + first) * K_PASS
+            source = concat_memory
             if kind == "w":
-                source, column = conv_w, first + (CHANNELS if half == "memory" else 0)
-            else:
-                source, column = concat_memory, first
-            rows = rows_pool.tile([P, TILES, K_CHUNK], BF16, tag="%s_rows" % kind)
+                source = conv_w
+                column += CHANNELS if half == "memory" else 0
+            if (c, kind) not in chunk_rows:
+                chunk_rows[c, kind] = rows_pool.tile([P, TILES, K_CHUNK], BF16, tag="%s_rows" % kind, name="rows")
             nc.sync.dma_start(
-                out=rows[:], in_=source[:, column : column + K_CHUNK].rearrange("(t p) k -> p t k", p=P)
+                out=chunk_rows[c, kind][:, :, first * K_PASS : (first + count) * K_PASS],
+                in_=source[:, column : column + count * K_PASS].rearrange("(t p) k -> p t k", p=P),
             )
-            chunk_rows[c, kind] = rows
 
         banks = {"next": 0, "count": TRANSPOSE_BANKS - 1}
 
@@ -120,24 +122,52 @@ def tile_memory_sup_pb_k_kernel(tc, query, concat_memory, conv_w, bn_gamma, bn_b
             chunk = range(c * CHUNK_PASSES, (c + 1) * CHUNK_PASSES)
             slabs = [s for i in chunk for s in slabs_multiplied(i)]
             slabs.extend(sorted(set(BATCH_SLABS + k * BANK_PLANES // SLAB_PLANES for i in chunk for k in banks_squared(i))))
-            for slab in slabs[:1]:
-                load_slab(slab)
-            load_rows(c, "w")
-            for slab in slabs[1:2]:
-                load_slab(slab)
-            if passes[c * CHUNK_PASSES][0] == "memory":
-                load_rows(c, "m")
-            for slab in slabs[2:]:
+            step = 1 if c == 0 else CHUNK_PASSES
+            for first in range(0, CHUNK_PASSES, step):
+                for kind in ("w", "m") if passes[c * CHUNK_PASSES][0] == "memory" else ("w",):
+                    for slab in slabs[:1]:
+                        load_slab(slab)
+                    slabs = slabs[1:]
+                    load_rows(c, kind, first, step)
+            for slab in slabs:
                 load_slab(slab)
 
-        def transpose_rows(rows, local, pair, grouped_words, copy):
+        ordered_of = {}
+
+        def order_engine(i, operand, pair):
+            if i <= GRAM_PASSES:
+                return None
+            if i < SQUARE_END:
+                return nc.vector.tensor_copy if operand == "w" and pair == 0 else None
+            if i < HALF_PASSES:
+                return nc.scalar.copy if operand == "w" else None
+            return nc.scalar.copy if pair == 0 or i % 2 == 1 else nc.vector.tensor_copy
+
+        def order_rows(i):
+            if i >= len(passes):
+                return
+            c, local = divmod(i, CHUNK_PASSES)
+            for operand in ("w", "m") if passes[i][0] == "memory" else ("w",):
+                for pair in range(TILES // 2):
+                    copy = order_engine(i, operand, pair)
+                    if copy is None:
+                        continue
+                    ordered = ordered_pool.tile([P, 2, 2, P], F32, tag="%s%d" % (operand, pair), name="ordered")
+                    words = chunk_rows[c, operand][:, 2 * pair : 2 * pair + 2, local * K_PASS : (local + 1) * K_PASS]
+                    copy(out=ordered[:], in_=words.bitcast(F32).rearrange("p t (w u) -> p t u w", u=2))
+                    ordered_of[i, operand, pair] = ordered
+
+        def transpose_rows(i, operand, pair, grouped_words, copy):
             bank = next_bank()
             for j in range(4):
-                t, u = 2 * pair + j // 2, j % 2
-                first = 2 * local * P
-                nc.tensor.transpose(
-                    bank[:, j, :], rows[:, t, :].bitcast(F32)[:, first + u : first + 2 * P : 2], ident[:]
-                )
+                t, u = divmod(j, 2)
+                if (i, operand, pair) in ordered_of:
+                    words = ordered_of[i, operand, pair][:, t, u, :]
+                else:
+                    c, local = divmod(i, CHUNK_PASSES)
+                    words = chunk_rows[c, operand][:, 2 * pair + t, :].bitcast(F32)
+                    words = words[:, 2 * P * local + u : 2 * P * (local + 1) : 2]
+                nc.tensor.transpose(bank[:, j, :], words, ident[:])
             copy(
                 out=grouped_words[:, 4 * P * pair : 4 * P * (pair + 1)].rearrange("p (t r u) -> p t r u", t=2, u=2),
                 in_=bank[:].rearrange("p (t u) r -> p t r u", u=2),
@@ -190,14 +220,16 @@ def tile_memory_sup_pb_k_kernel(tc, query, concat_memory, conv_w, bn_gamma, bn_b
                 start=True,
                 stop=True,
             )
+            floored = scratch.tile([P, PIXELS], F32, tag="norms")
+            nc.vector.tensor_scalar_max(
+                out=floored[:], in0=bank[:, 0:2, :].rearrange("p h r -> p (h r)"), scalar1=L2_EPS * L2_EPS
+            )
             norm = scratch.tile([P, PIXELS], F32, tag="norms")
-            nc.scalar.sqrt(out=norm[:], in_=bank[:, 0:2, :].rearrange("p h r -> p (h r)"))
+            nc.scalar.sqrt(out=norm[:], in_=floored[:])
             scales_of["norm"] = norm
 
         def batch_0_scales_finish():
-            floored = scratch.tile([P, PIXELS], F32, tag="norms")
-            nc.vector.tensor_scalar_max(out=floored[:], in0=scales_of["norm"][:], scalar1=L2_EPS)
-            nc.vector.reciprocal(out=inv_norm[:, 0, :], in_=floored[:])
+            nc.vector.reciprocal(out=inv_norm[:, 0, :], in_=scales_of["norm"][:])
 
         def batch_1_scales_start():
             total = scratch.tile([P, 2], F32, tag="total")
@@ -260,13 +292,11 @@ def tile_memory_sup_pb_k_kernel(tc, query, concat_memory, conv_w, bn_gamma, bn_b
             c, local = divmod(i, CHUNK_PASSES)
             if local == 0:
                 load_for_chunk(c + AHEAD)
-            w_rows = chunk_rows[c, "w"]
             grouped = work.tile([P, 4 * (OUT_CH + ROWS)], BF16, tag="grouped", align_bytes=64)
             words = grouped[:].bitcast(F32)
-            to_copy = [(w_rows, pair, words[:, 0 : 2 * OUT_CH]) for pair in range(TILES // 2)]
+            to_copy = [("w", pair, words[:, 0 : 2 * OUT_CH]) for pair in range(TILES // 2)]
             if kind == "memory":
-                m_rows = chunk_rows[c, "m"]
-                to_copy.extend([(m_rows, pair, words[:, 2 * OUT_CH : 2 * (OUT_CH + ROWS)]) for pair in range(TILES // 2)])
+                to_copy.extend([("m", pair, words[:, 2 * OUT_CH : 2 * (OUT_CH + ROWS)]) for pair in range(TILES // 2)])
             to_multiply = list(slabs_multiplied(i))
             to_square = list(banks_squared(i))
             if i == SQUARE_END:
@@ -276,9 +306,9 @@ def tile_memory_sup_pb_k_kernel(tc, query, concat_memory, conv_w, bn_gamma, bn_b
                     multiply_slab(to_multiply[k])
                 if k < len(to_square):
                     square_bank(to_square[k])
-                rows, pair, half = to_copy[k]
-                on_vector = i < SQUARE_END and rows is w_rows
-                transpose_rows(rows, local, pair, half, nc.vector.tensor_copy if on_vector else nc.scalar.copy)
+                operand, pair, half = to_copy[k]
+                on_vector = GRAM_PASSES <= i < SQUARE_END and operand == "w"
+                transpose_rows(i, operand, pair, half, nc.vector.tensor_copy if on_vector else nc.scalar.copy)
             if i == GRAM_PASSES - 1:
                 batch_0_scales_start()
             if i == GRAM_PASSES:
@@ -292,7 +322,7 @@ def tile_memory_sup_pb_k_kernel(tc, query, concat_memory, conv_w, bn_gamma, bn_b
             elif i < SQUARE_END:
                 count = SHARED_SLICES
             elif kind == "memory":
-                count = FREE_SLICES
+                count = FREE_SLICES - (i + 1) % 2
             else:
                 count = 1
             slices = slices_left[:count]
@@ -325,11 +355,53 @@ def tile_memory_sup_pb_k_kernel(tc, query, concat_memory, conv_w, bn_gamma, bn_b
                 stop=(i == len(passes) - 1),
             )
 
+        mean_var = const.tile([P, TILES, 2], F32)
+        std = const.tile([P, TILES], F32)
+        inv_std = const.tile([P, TILES], F32)
+        gain = const.tile([P, TILES], F32)
+        mean_gain = const.tile([P, TILES], F32)
+        shift = const.tile([P, TILES], F32)
+        out_tiles = out.rearrange("b (t p) h w -> t p b (h w)", p=P)
+
+        def tile_statistics(t):
+            stats = const.tile([P, 6], F32, name="stats%d" % t)
+            nc.vector.bn_stats(out=stats[:], in_=acc[t][:])
+            nc.vector.bn_aggr(out=mean_var[:, t, :], in_=stats[:])
+            nc.scalar.activation(out=std[:, t : t + 1], in_=mean_var[:, t, 1:2], func=ACT.Sqrt, bias=BN_EPS)
+
+        def gain_and_shift(tiles):
+            cols = slice(tiles.start, tiles.stop)
+            nc.vector.reciprocal(out=inv_std[:, cols], in_=std[:, cols])
+            nc.vector.tensor_tensor(out=gain[:, cols], in0=gamma_beta[:, cols], in1=inv_std[:, cols], op=ALU.mult)
+            nc.vector.tensor_tensor(out=mean_gain[:, cols], in0=mean_var[:, cols, 0], in1=gain[:, cols], op=ALU.mult)
+            beta = gamma_beta[:, TILES + tiles.start : TILES + tiles.stop]
+            nc.vector.tensor_tensor(out=shift[:, cols], in0=beta, in1=mean_gain[:, cols], op=ALU.subtract)
+
+        def store_tile(t):
+            result = const.tile([P, BATCH, PIXELS], F32, name="result%d" % t)
+            flat = result[:].rearrange("p b n -> p (b n)")
+            if t == 1:
+                nc.vector.tensor_scalar(
+                    out=flat,
+                    in0=acc[t][:],
+                    scalar1=gain[:, t : t + 1],
+                    scalar2=shift[:, t : t + 1],
+                    op0=ALU.mult,
+                    op1=ALU.add,
+                )
+                nc.vector.tensor_scalar_max(out=flat, in0=flat, scalar1=0.0)
+            else:
+                nc.scalar.activation(
+                    out=flat, in_=acc[t][:], func=ACT.Relu, scale=gain[:, t : t + 1], bias=shift[:, t : t + 1]
+                )
+            nc.sync.dma_start(out=out_tiles[t], in_=result[:])
+
         for c in range(AHEAD):
             load_for_chunk(c)
 
         with tc.manual_schedule():
             for i in range(len(passes)):
+                order_rows(i + 1)
                 slices = prepare(i)
                 if i >= 1:
                     quantise(i - 1)
@@ -343,32 +415,8 @@ def tile_memory_sup_pb_k_kernel(tc, query, concat_memory, conv_w, bn_gamma, bn_b
             for t in range(TILES):
                 for i in range(len(passes) - LAG, len(passes)):
                     multiply(i, t)
-
-        stats = const.tile([P, TILES, 6], F32)
-        mean_var = const.tile([P, TILES, 2], F32)
-        for t in range(TILES):
-            nc.vector.bn_stats(out=stats[:, t, :], in_=acc[t][:])
-            nc.vector.bn_aggr(out=mean_var[:, t, :], in_=stats[:, t, :])
-        var_eps = const.tile([P, TILES], F32)
-        nc.vector.tensor_scalar_add(out=var_eps[:], in0=mean_var[:, :, 1], scalar1=BN_EPS)
-        std = const.tile([P, TILES], F32)
-        nc.scalar.sqrt(out=std[:], in_=var_eps[:])
-        inv_std = const.tile([P, TILES], F32)
-        nc.vector.reciprocal(out=inv_std[:], in_=std[:])
-        gain = const.tile([P, TILES], F32)
-        nc.vector.tensor_tensor(out=gain[:], in0=gamma_beta[:, 0:TILES], in1=inv_std[:], op=ALU.mult)
-        mean_gain = const.tile([P, TILES], F32)
-        nc.vector.tensor_tensor(out=mean_gain[:], in0=mean_var[:, :, 0], in1=gain[:], op=ALU.mult)
-        shift = const.tile([P, TILES], F32)
-        nc.vector.tensor_tensor(out=shift[:], in0=gamma_beta[:, TILES : 2 * TILES], in1=mean_gain[:], op=ALU.subtract)
-        out_tiles = out.rearrange("b (t p) h w -> t p b (h w)", p=P)
-        for t in range(TILES):
-            result = scratch.tile([P, BATCH, PIXELS], F32, tag="result")
-            nc.scalar.activation(
-                out=result[:].rearrange("p b n -> p (b n)"),
-                in_=acc[t][:],
-                func=ACT.Relu,
-                scale=gain[:, t : t + 1],
-                bias=shift[:, t : t + 1],
-            )
-            nc.sync.dma_start(out=out_tiles[t], in_=result[:])
+                tile_statistics(t)
+            for tiles in (range(0, TILES - 1), range(TILES - 1, TILES)):
+                gain_and_shift(tiles)
+            for t in range(TILES):
+                store_tile(t)

@@ -28,15 +28,13 @@ BANK_PLANES = 4
 BATCH_BANKS = PLANES // BANK_PLANES
 SLAB_PLANES = 8
 BATCH_SLABS = PLANES // SLAB_PLANES
-GRAM_PASSES = 3
-GRAM_SLABS = -(-BATCH_SLABS // GRAM_PASSES)
-SQUARE_BANKS = 2
-SQUARE_PASSES = BATCH_BANKS // SQUARE_BANKS
-SQUARE_END = GRAM_PASSES + SQUARE_PASSES
+FIRST_PASSES = 4
+GRAM_SLABS = 2
+GRAM_END = FIRST_PASSES + BATCH_SLABS // GRAM_SLABS
+SQUARE_PASSES = BATCH_BANKS // 2
+SQUARE_END = GRAM_END + SQUARE_PASSES
 RUN = 4
 TRANSPOSE_BANKS = 4
-SHARED_SLICES = 1
-FREE_SLICES = 2
 AHEAD = 2
 LAG = 2
 L2_EPS = 1e-12
@@ -69,7 +67,7 @@ def tile_memory_sup_pb_k_kernel(tc, query, concat_memory, conv_w, bn_gamma, bn_b
         make_identity(nc, ident[:])
 
         q_sb = const.tile([P, BATCH, PLANES, PIXELS], BF16)
-        sum_sq = const.tile([P, 2, BATCH_BANKS], F32)
+        sum_sq = const.tile([P, 2, SQUARE_PASSES], F32)
         inv_norm = const.tile([P, BATCH, PIXELS], F32)
         q_codes = const.tile([P, HALF_PASSES, ROWS], U32, align_bytes=64)
         q_scales = const.tile([P, HALF_PASSES, ROWS], U8, align_bytes=64)
@@ -99,49 +97,50 @@ def tile_memory_sup_pb_k_kernel(tc, query, concat_memory, conv_w, bn_gamma, bn_b
                 in_=source[:, column : column + count * K_PASS].rearrange("(t p) k -> p t k", p=P),
             )
 
-        banks = {"next": 0, "count": TRANSPOSE_BANKS - 1}
+        banks = {"next": 0, "count": TRANSPOSE_BANKS}
 
         def next_bank():
-            k = banks["next"]
-            banks["next"] = (k + 1) % banks["count"]
+            k = banks["next"] % banks["count"]
+            banks["next"] = k + 1
             return bank_pool.tile([P, 4, P], F32, tag="bank%d" % k, name="bank%d" % k)
 
         def slabs_multiplied(i):
-            if i < GRAM_PASSES:
-                return range(GRAM_SLABS * i, min(GRAM_SLABS * (i + 1), BATCH_SLABS))
+            if FIRST_PASSES <= i < GRAM_END:
+                return range(GRAM_SLABS * (i - FIRST_PASSES), GRAM_SLABS * (i - FIRST_PASSES + 1))
             return range(0)
 
         def banks_squared(i):
-            if GRAM_PASSES <= i < SQUARE_END:
-                return range(SQUARE_BANKS * (i - GRAM_PASSES), SQUARE_BANKS * (i - GRAM_PASSES + 1))
+            if GRAM_END <= i < SQUARE_END:
+                return range(BATCH_BANKS // 2 + i - GRAM_END, BATCH_BANKS // 2 + i - GRAM_END + 1)
             return range(0)
 
         def load_for_chunk(c):
             if c * CHUNK_PASSES >= len(passes):
                 return
-            chunk = range(c * CHUNK_PASSES, (c + 1) * CHUNK_PASSES)
-            slabs = [s for i in chunk for s in slabs_multiplied(i)]
-            slabs.extend(sorted(set(BATCH_SLABS + k * BANK_PLANES // SLAB_PLANES for i in chunk for k in banks_squared(i))))
-            step = 1 if c == 0 else CHUNK_PASSES
+            step = 1 if c < 2 else CHUNK_PASSES
             for first in range(0, CHUNK_PASSES, step):
-                for kind in ("w", "m") if passes[c * CHUNK_PASSES][0] == "memory" else ("w",):
-                    for slab in slabs[:1]:
-                        load_slab(slab)
-                    slabs = slabs[1:]
-                    load_rows(c, kind, first, step)
-            for slab in slabs:
-                load_slab(slab)
+                part = range(c * CHUNK_PASSES + first, c * CHUNK_PASSES + first + step)
+                slabs = [s for i in part for s in slabs_multiplied(i)]
+                for i in part:
+                    for k in banks_squared(i):
+                        if k % 2 == 0:
+                            slabs.extend([BATCH_SLABS + (k - BATCH_BANKS // 2) // 2, BATCH_SLABS + k // 2])
+                load_rows(c, "w", first, step)
+                for slab in slabs[: len(slabs) // 2]:
+                    load_slab(slab)
+                if passes[c * CHUNK_PASSES][0] == "memory":
+                    load_rows(c, "m", first, step)
+                for slab in slabs[len(slabs) // 2 :]:
+                    load_slab(slab)
 
         ordered_of = {}
 
         def order_engine(i, operand, pair):
-            if i <= GRAM_PASSES:
+            if i < GRAM_END:
+                return nc.vector.tensor_copy
+            if i < HALF_PASSES or pair == 1:
                 return None
-            if i < SQUARE_END:
-                return nc.vector.tensor_copy if operand == "w" and pair == 0 else None
-            if i < HALF_PASSES:
-                return nc.scalar.copy if operand == "w" else None
-            return nc.scalar.copy if pair == 0 or i % 2 == 1 else nc.vector.tensor_copy
+            return nc.scalar.copy
 
         def order_rows(i):
             if i >= len(passes):
@@ -157,18 +156,18 @@ def tile_memory_sup_pb_k_kernel(tc, query, concat_memory, conv_w, bn_gamma, bn_b
                     copy(out=ordered[:], in_=words.bitcast(F32).rearrange("p t (w u) -> p t u w", u=2))
                     ordered_of[i, operand, pair] = ordered
 
-        def transpose_rows(i, operand, pair, grouped_words, copy):
+        def transpose_rows(i, operand, pair, grouped_words):
+            c, local = divmod(i, CHUNK_PASSES)
             bank = next_bank()
             for j in range(4):
                 t, u = divmod(j, 2)
                 if (i, operand, pair) in ordered_of:
                     words = ordered_of[i, operand, pair][:, t, u, :]
                 else:
-                    c, local = divmod(i, CHUNK_PASSES)
                     words = chunk_rows[c, operand][:, 2 * pair + t, :].bitcast(F32)
                     words = words[:, 2 * P * local + u : 2 * P * (local + 1) : 2]
                 nc.tensor.transpose(bank[:, j, :], words, ident[:])
-            copy(
+            nc.scalar.copy(
                 out=grouped_words[:, 4 * P * pair : 4 * P * (pair + 1)].rearrange("p (t r u) -> p t r u", t=2, u=2),
                 in_=bank[:].rearrange("p (t u) r -> p t r u", u=2),
             )
@@ -184,31 +183,36 @@ def tile_memory_sup_pb_k_kernel(tc, query, concat_memory, conv_w, bn_gamma, bn_b
                     out=squares[:],
                     in_=by_parity[:, h],
                     func=ACT.Square,
-                    accum_out=sum_sq[:, h, k : k + 1],
+                    accum_out=sum_sq[:, h, k - BATCH_BANKS // 2 : k - BATCH_BANKS // 2 + 1],
                 )
 
-        gram = bank_pool.tile([P, 2, P], F32, tag="bank%d" % (TRANSPOSE_BANKS - 1), name="gram")
+        gram_of = {}
+
+        def multiply_planes(b, planes, count):
+            if b not in gram_of:
+                banks["count"] = TRANSPOSE_BANKS - 1
+                gram_of[b] = bank_pool.tile([P, 2, P], F32, tag="bank%d" % (TRANSPOSE_BANKS - 1), name="gram")
+            for plane in planes:
+                for h in range(2):
+                    pixels = q_sb[:, b, plane, h * P : (h + 1) * P] if b == 0 else q_sb[:, b, plane, h::2]
+                    nc.tensor.matmul(
+                        gram_of[b][:, h, :],
+                        lhsT=pixels,
+                        rhs=pixels,
+                        start=(plane == 0 and h == 0),
+                        stop=(plane == count - 1 and h == 1),
+                    )
 
         def multiply_slab(slab):
-            for plane in range(slab * SLAB_PLANES, (slab + 1) * SLAB_PLANES):
-                for h in range(2):
-                    half = q_sb[:, 0, plane, h * P : (h + 1) * P]
-                    nc.tensor.matmul(
-                        gram[:, h, :],
-                        lhsT=half,
-                        rhs=half,
-                        start=(plane == 0 and h == 0),
-                        stop=(plane == PLANES - 1 and h == 1),
-                    )
+            multiply_planes(0, range(slab * SLAB_PLANES, (slab + 1) * SLAB_PLANES), PLANES)
 
         scales_of = {}
 
         def batch_0_scales_start():
             diagonal = scratch.tile([P, 2, P], F32, tag="diagonal")
             nc.vector.tensor_tensor(
-                out=diagonal[:], in0=gram[:], in1=ident[:].unsqueeze(1).to_broadcast([P, 2, P]), op=ALU.mult
+                out=diagonal[:], in0=gram_of[0][:], in1=ident[:].unsqueeze(1).to_broadcast([P, 2, P]), op=ALU.mult
             )
-            banks["count"] = TRANSPOSE_BANKS
             scales_of["diagonal"] = diagonal
 
         def batch_0_scales_spread():
@@ -234,25 +238,41 @@ def tile_memory_sup_pb_k_kernel(tc, query, concat_memory, conv_w, bn_gamma, bn_b
         def batch_1_scales_start():
             total = scratch.tile([P, 2], F32, tag="total")
             nc.vector.tensor_reduce(out=total[:], in_=sum_sq[:], axis=AXIS.X, op=ALU.add)
-            floored = scratch.tile([P, 2], F32, tag="floored")
-            nc.vector.tensor_scalar_max(out=floored[:], in0=total[:], scalar1=L2_EPS * L2_EPS)
-            norm = scratch.tile([P, 2], F32, tag="norm")
-            nc.scalar.sqrt(out=norm[:], in_=floored[:])
-            inv = scratch.tile([P, 2], F32, tag="inv")
-            nc.vector.reciprocal(out=inv[:], in_=norm[:])
-            repeated = scratch.tile([P, 2, P], F32, tag="repeated")
+            products = scratch.tile([P, 2, P], F32, tag="diagonal", name="products")
+            nc.vector.tensor_tensor(
+                out=products[:], in0=gram_of[1][:], in1=ident[:].unsqueeze(1).to_broadcast([P, 2, P]), op=ALU.mult
+            )
+            diagonal = scratch.tile([P, 2, P], F32, tag="diagonal", name="diagonal")
             for h in range(2):
-                nc.vector.tensor_scalar_mul(out=repeated[:, h, :], in0=ones[:], scalar1=inv[:, h : h + 1])
-            scales_of["repeated"] = repeated
+                nc.vector.scalar_tensor_tensor(
+                    out=diagonal[:, h, :],
+                    in0=ident[:],
+                    scalar=total[:, h : h + 1],
+                    in1=products[:, h, :],
+                    op0=ALU.mult,
+                    op1=ALU.add,
+                )
+            banks["count"] = TRANSPOSE_BANKS
+            scales_of["diagonal"] = diagonal
 
         def batch_1_scales_finish():
             bank = next_bank()
-            for h in range(2):
-                nc.tensor.transpose(bank[:, h, :], scales_of["repeated"][:, h, :], ident[:])
-            nc.vector.tensor_copy(
-                out=inv_norm[:, 1, :].rearrange("p (w h) -> p w h", h=2),
-                in_=bank[:, 0:2, :].rearrange("p h w -> p w h"),
+            nc.tensor.matmul(
+                bank[:, 0:2, :].rearrange("p h r -> p (h r)"),
+                lhsT=ones[:],
+                rhs=scales_of["diagonal"][:].rearrange("p h r -> p (h r)"),
+                start=True,
+                stop=True,
             )
+            floored = scratch.tile([P, PIXELS], F32, tag="norms")
+            nc.vector.tensor_scalar_max(
+                out=floored[:].rearrange("p (r h) -> p r h", h=2),
+                in0=bank[:, 0:2, :].rearrange("p h r -> p r h"),
+                scalar1=L2_EPS * L2_EPS,
+            )
+            norm = scratch.tile([P, PIXELS], F32, tag="norms")
+            nc.scalar.sqrt(out=norm[:], in_=floored[:])
+            nc.vector.reciprocal(out=inv_norm[:, 1, :], in_=norm[:])
 
         def transpose_gamma_beta():
             gb_f32 = const.tile([P, P], F32)
@@ -302,32 +322,28 @@ def tile_memory_sup_pb_k_kernel(tc, query, concat_memory, conv_w, bn_gamma, bn_b
             if i == SQUARE_END:
                 batch_1_scales_start()
             for k in range(len(to_copy)):
-                if k < len(to_multiply):
-                    multiply_slab(to_multiply[k])
                 if k < len(to_square):
                     square_bank(to_square[k])
                 operand, pair, half = to_copy[k]
-                on_vector = GRAM_PASSES <= i < SQUARE_END and operand == "w"
-                transpose_rows(i, operand, pair, half, nc.vector.tensor_copy if on_vector else nc.scalar.copy)
-            if i == GRAM_PASSES - 1:
+                transpose_rows(i, operand, pair, half)
+                if pair == TILES // 2 - 1:
+                    for slab in to_multiply[:1] if operand == "w" else to_multiply[1:]:
+                        multiply_slab(slab)
+                    if operand == "w" and GRAM_END <= i < SQUARE_END:
+                        first = BANK_PLANES * (i - GRAM_END)
+                        multiply_planes(1, range(first, first + BANK_PLANES), PLANES // 2)
+            if i == GRAM_END - 1:
                 batch_0_scales_start()
-            if i == GRAM_PASSES:
+            if i == GRAM_END:
                 batch_0_scales_finish()
             if i == SQUARE_END:
                 batch_1_scales_finish()
                 transpose_gamma_beta()
             grouped_of[i] = grouped
-            if i < GRAM_PASSES:
-                count = 0
-            elif i < SQUARE_END:
-                count = SHARED_SLICES
-            elif kind == "memory":
-                count = FREE_SLICES - (i + 1) % 2
-            else:
-                count = 1
+            count = 0 if i < GRAM_END else 2 if i <= SQUARE_END else 1
             slices = slices_left[:count]
             slices_left[:] = slices_left[count:]
-            return normalise(slices)
+            return slices
 
         def quantise(i):
             width = OUT_CH + (ROWS if passes[i][0] == "memory" else 0)
@@ -400,17 +416,22 @@ def tile_memory_sup_pb_k_kernel(tc, query, concat_memory, conv_w, bn_gamma, bn_b
             load_for_chunk(c)
 
         with tc.manual_schedule():
+            order_rows(0)
+            made = []
             for i in range(len(passes)):
-                order_rows(i + 1)
+                if i + 1 < len(passes):
+                    order_rows(i + 1)
                 slices = prepare(i)
                 if i >= 1:
                     quantise(i - 1)
-                quantise_slices(slices)
+                quantise_slices(made)
+                made = normalise(slices)
                 if i >= LAG:
                     for t in range(TILES):
                         multiply(i - LAG, t)
-                if i == GRAM_PASSES - 1:
+                if i == GRAM_END - 1:
                     batch_0_scales_spread()
+            quantise_slices(made)
             quantise(len(passes) - 1)
             for t in range(TILES):
                 for i in range(len(passes) - LAG, len(passes)):

@@ -28,7 +28,7 @@ BANK_PLANES = 4
 BATCH_BANKS = PLANES // BANK_PLANES
 SLAB_PLANES = 8
 BATCH_SLABS = PLANES // SLAB_PLANES
-FIRST_PASSES = 4
+FIRST_PASSES = 3
 GRAM_SLABS = 2
 GRAM_END = FIRST_PASSES + BATCH_SLABS // GRAM_SLABS
 SQUARE_PASSES = BATCH_BANKS // 2
@@ -92,10 +92,16 @@ def tile_memory_sup_pb_k_kernel(tc, query, concat_memory, conv_w, bn_gamma, bn_b
                 column += CHANNELS if half == "memory" else 0
             if (c, kind) not in chunk_rows:
                 chunk_rows[c, kind] = rows_pool.tile([P, TILES, K_CHUNK], BF16, tag="%s_rows" % kind, name="rows")
-            nc.sync.dma_start(
-                out=chunk_rows[c, kind][:, :, first * K_PASS : (first + count) * K_PASS],
-                in_=source[:, column : column + count * K_PASS].rearrange("(t p) k -> p t k", p=P),
-            )
+            parts = 2 if c == 0 and first == 0 and kind == "w" else 1
+            size = TILES // parts
+            for part in range(parts):
+                tiles = slice(size * part, size * (part + 1))
+                nc.sync.dma_start(
+                    out=chunk_rows[c, kind][:, tiles, first * K_PASS : (first + count) * K_PASS],
+                    in_=source[tiles.start * P : tiles.stop * P, column : column + count * K_PASS].rearrange(
+                        "(t p) k -> p t k", p=P
+                    ),
+                )
 
         banks = {"next": 0, "count": TRANSPOSE_BANKS}
 
@@ -136,6 +142,8 @@ def tile_memory_sup_pb_k_kernel(tc, query, concat_memory, conv_w, bn_gamma, bn_b
         ordered_of = {}
 
         def order_engine(i, operand, pair):
+            if i == 0 and operand == "w":
+                return None
             if i < GRAM_END:
                 return nc.vector.tensor_copy
             if i < HALF_PASSES or pair == 1:
@@ -208,75 +216,51 @@ def tile_memory_sup_pb_k_kernel(tc, query, concat_memory, conv_w, bn_gamma, bn_b
 
         scales_of = {}
 
-        def batch_0_scales_start():
-            diagonal = scratch.tile([P, 2, P], F32, tag="diagonal")
+        def pixel_scales_start(b):
+            products = scratch.tile([P, 2, P], F32, tag="products", name="products")
             nc.vector.tensor_tensor(
-                out=diagonal[:], in0=gram_of[0][:], in1=ident[:].unsqueeze(1).to_broadcast([P, 2, P]), op=ALU.mult
+                out=products[:], in0=gram_of[b][:], in1=ident[:].unsqueeze(1).to_broadcast([P, 2, P]), op=ALU.mult
             )
-            scales_of["diagonal"] = diagonal
-
-        def batch_0_scales_spread():
-            bank = next_bank()
-            nc.tensor.matmul(
-                bank[:, 0:2, :].rearrange("p h r -> p (h r)"),
-                lhsT=ones[:],
-                rhs=scales_of["diagonal"][:].rearrange("p h r -> p (h r)"),
-                start=True,
-                stop=True,
-            )
-            floored = scratch.tile([P, PIXELS], F32, tag="norms")
-            nc.vector.tensor_scalar_max(
-                out=floored[:], in0=bank[:, 0:2, :].rearrange("p h r -> p (h r)"), scalar1=L2_EPS * L2_EPS
-            )
-            norm = scratch.tile([P, PIXELS], F32, tag="norms")
+            total = scratch.tile([P, 2], F32, tag="total", name="total")
+            nc.vector.tensor_reduce(out=total[:], in_=products[:], axis=AXIS.X, op=ALU.add)
+            if b == 1:
+                squared = scratch.tile([P, 2], F32, tag="squared", name="squared")
+                nc.vector.tensor_reduce(out=squared[:], in_=sum_sq[:], axis=AXIS.X, op=ALU.add)
+                both = scratch.tile([P, 2], F32, tag="both", name="both")
+                nc.vector.tensor_tensor(out=both[:], in0=total[:], in1=squared[:], op=ALU.add)
+                total = both
+                banks["count"] = TRANSPOSE_BANKS
+            floored = scratch.tile([P, 2], F32, tag="floored", name="floored")
+            nc.vector.tensor_scalar_max(out=floored[:], in0=total[:], scalar1=L2_EPS * L2_EPS)
+            norm = scratch.tile([P, 2], F32, tag="norm", name="norm")
             nc.scalar.sqrt(out=norm[:], in_=floored[:])
-            scales_of["norm"] = norm
-
-        def batch_0_scales_finish():
-            nc.vector.reciprocal(out=inv_norm[:, 0, :], in_=scales_of["norm"][:])
-
-        def batch_1_scales_start():
-            total = scratch.tile([P, 2], F32, tag="total")
-            nc.vector.tensor_reduce(out=total[:], in_=sum_sq[:], axis=AXIS.X, op=ALU.add)
-            products = scratch.tile([P, 2, P], F32, tag="diagonal", name="products")
-            nc.vector.tensor_tensor(
-                out=products[:], in0=gram_of[1][:], in1=ident[:].unsqueeze(1).to_broadcast([P, 2, P]), op=ALU.mult
-            )
+            inv = scratch.tile([P, 2], F32, tag="inv", name="inv")
+            nc.vector.reciprocal(out=inv[:], in_=norm[:])
             diagonal = scratch.tile([P, 2, P], F32, tag="diagonal", name="diagonal")
             for h in range(2):
-                nc.vector.scalar_tensor_tensor(
-                    out=diagonal[:, h, :],
-                    in0=ident[:],
-                    scalar=total[:, h : h + 1],
-                    in1=products[:, h, :],
-                    op0=ALU.mult,
-                    op1=ALU.add,
-                )
-            banks["count"] = TRANSPOSE_BANKS
-            scales_of["diagonal"] = diagonal
+                nc.vector.tensor_scalar_mul(out=diagonal[:, h, :], in0=ident[:], scalar1=inv[:, h : h + 1])
+            scales_of[b] = diagonal
 
-        def batch_1_scales_finish():
+        def pixel_scales_spread(b):
             bank = next_bank()
             nc.tensor.matmul(
                 bank[:, 0:2, :].rearrange("p h r -> p (h r)"),
                 lhsT=ones[:],
-                rhs=scales_of["diagonal"][:].rearrange("p h r -> p (h r)"),
+                rhs=scales_of[b][:].rearrange("p h r -> p (h r)"),
                 start=True,
                 stop=True,
             )
-            floored = scratch.tile([P, PIXELS], F32, tag="norms")
-            nc.vector.tensor_scalar_max(
-                out=floored[:].rearrange("p (r h) -> p r h", h=2),
-                in0=bank[:, 0:2, :].rearrange("p h r -> p r h"),
-                scalar1=L2_EPS * L2_EPS,
-            )
-            norm = scratch.tile([P, PIXELS], F32, tag="norms")
-            nc.scalar.sqrt(out=norm[:], in_=floored[:])
-            nc.vector.reciprocal(out=inv_norm[:, 1, :], in_=norm[:])
+            if b == 0:
+                nc.vector.tensor_copy(out=inv_norm[:, b, :], in_=bank[:, 0:2, :].rearrange("p h r -> p (h r)"))
+            else:
+                nc.vector.tensor_copy(
+                    out=inv_norm[:, b, :].rearrange("p (r h) -> p r h", h=2),
+                    in_=bank[:, 0:2, :].rearrange("p h r -> p r h"),
+                )
+
+        gb_f32 = const.tile([P, P], F32)
 
         def transpose_gamma_beta():
-            gb_f32 = const.tile([P, P], F32)
-            nc.vector.tensor_copy(out=gb_f32[:], in_=gb_rows[:])
             bank = next_bank()
             nc.tensor.transpose(bank[:, 0, :], gb_f32[:], ident[:])
             nc.vector.tensor_copy(out=gamma_beta[:], in_=bank[:, 0, 0 : 2 * TILES])
@@ -304,6 +288,7 @@ def tile_memory_sup_pb_k_kernel(tc, query, concat_memory, conv_w, bn_gamma, bn_b
                 pixels = slice(b * PIXELS, (b + 1) * PIXELS)
                 nc.vector.quantize_mx(out=q_codes[:, g, pixels].bitcast(FP8X4), scales=q_scales[:, g, pixels], in_=q_flat)
 
+        scales_due = {GRAM_END: 0, SQUARE_END: 1}
         grouped_of = {}
         operands_of = {}
 
@@ -319,28 +304,28 @@ def tile_memory_sup_pb_k_kernel(tc, query, concat_memory, conv_w, bn_gamma, bn_b
                 to_copy.extend([("m", pair, words[:, 2 * OUT_CH : 2 * (OUT_CH + ROWS)]) for pair in range(TILES // 2)])
             to_multiply = list(slabs_multiplied(i))
             to_square = list(banks_squared(i))
-            if i == SQUARE_END:
-                batch_1_scales_start()
             for k in range(len(to_copy)):
                 if k < len(to_square):
                     square_bank(to_square[k])
                 operand, pair, half = to_copy[k]
                 transpose_rows(i, operand, pair, half)
+                if k == 0 and i in scales_due:
+                    pixel_scales_spread(scales_due[i])
+                    if i == SQUARE_END:
+                        transpose_gamma_beta()
                 if pair == TILES // 2 - 1:
                     for slab in to_multiply[:1] if operand == "w" else to_multiply[1:]:
                         multiply_slab(slab)
                     if operand == "w" and GRAM_END <= i < SQUARE_END:
                         first = BANK_PLANES * (i - GRAM_END)
                         multiply_planes(1, range(first, first + BANK_PLANES), PLANES // 2)
-            if i == GRAM_END - 1:
-                batch_0_scales_start()
-            if i == GRAM_END:
-                batch_0_scales_finish()
-            if i == SQUARE_END:
-                batch_1_scales_finish()
-                transpose_gamma_beta()
             grouped_of[i] = grouped
-            count = 0 if i < GRAM_END else 2 if i <= SQUARE_END else 1
+            if i < GRAM_END:
+                count = 0
+            elif i <= SQUARE_END:
+                count = 2
+            else:
+                count = 1
             slices = slices_left[:count]
             slices_left[:] = slices_left[count:]
             return slices
@@ -379,19 +364,23 @@ def tile_memory_sup_pb_k_kernel(tc, query, concat_memory, conv_w, bn_gamma, bn_b
         shift = const.tile([P, TILES], F32)
         out_tiles = out.rearrange("b (t p) h w -> t p b (h w)", p=P)
 
-        def tile_statistics(t):
-            stats = const.tile([P, 6], F32, name="stats%d" % t)
-            nc.vector.bn_stats(out=stats[:], in_=acc[t][:])
-            nc.vector.bn_aggr(out=mean_var[:, t, :], in_=stats[:])
+        stats = const.tile([P, TILES, 6], F32)
+
+        def tile_deviation(t):
+            nc.vector.bn_aggr(out=mean_var[:, t, :], in_=stats[:, t, :])
             nc.scalar.activation(out=std[:, t : t + 1], in_=mean_var[:, t, 1:2], func=ACT.Sqrt, bias=BN_EPS)
 
-        def gain_and_shift(tiles):
-            cols = slice(tiles.start, tiles.stop)
-            nc.vector.reciprocal(out=inv_std[:, cols], in_=std[:, cols])
-            nc.vector.tensor_tensor(out=gain[:, cols], in0=gamma_beta[:, cols], in1=inv_std[:, cols], op=ALU.mult)
-            nc.vector.tensor_tensor(out=mean_gain[:, cols], in0=mean_var[:, cols, 0], in1=gain[:, cols], op=ALU.mult)
-            beta = gamma_beta[:, TILES + tiles.start : TILES + tiles.stop]
-            nc.vector.tensor_tensor(out=shift[:, cols], in0=beta, in1=mean_gain[:, cols], op=ALU.subtract)
+        def gains_and_shifts(groups):
+            columns = [slice(tiles.start, tiles.stop) for tiles in groups]
+            for cols in columns:
+                nc.vector.reciprocal(out=inv_std[:, cols], in_=std[:, cols])
+            for cols in columns:
+                nc.vector.tensor_tensor(out=gain[:, cols], in0=gamma_beta[:, cols], in1=inv_std[:, cols], op=ALU.mult)
+            for cols in columns:
+                nc.vector.tensor_tensor(out=mean_gain[:, cols], in0=mean_var[:, cols, 0], in1=gain[:, cols], op=ALU.mult)
+            for cols in columns:
+                beta = gamma_beta[:, TILES + cols.start : TILES + cols.stop]
+                nc.vector.tensor_tensor(out=shift[:, cols], in0=beta, in1=mean_gain[:, cols], op=ALU.subtract)
 
         def store_tile(t):
             result = const.tile([P, BATCH, PIXELS], F32, name="result%d" % t)
@@ -424,20 +413,28 @@ def tile_memory_sup_pb_k_kernel(tc, query, concat_memory, conv_w, bn_gamma, bn_b
                 slices = prepare(i)
                 if i >= 1:
                     quantise(i - 1)
+                if i == 1:
+                    nc.vector.tensor_copy(out=gb_f32[:], in_=gb_rows[:])
                 quantise_slices(made)
+                if i + 1 in scales_due:
+                    pixel_scales_start(scales_due[i + 1])
                 made = normalise(slices)
-                if i >= LAG:
+                if i < HALF_PASSES:
+                    due = [i - LAG] if i >= LAG else []
+                else:
+                    due = [i - LAG - 1, i - LAG] if i % 2 == 1 else []
+                for k in due:
                     for t in range(TILES):
-                        multiply(i - LAG, t)
-                if i == GRAM_END - 1:
-                    batch_0_scales_spread()
+                        multiply(k, t)
             quantise_slices(made)
             quantise(len(passes) - 1)
             for t in range(TILES):
                 for i in range(len(passes) - LAG, len(passes)):
                     multiply(i, t)
-                tile_statistics(t)
-            for tiles in (range(0, TILES - 1), range(TILES - 1, TILES)):
-                gain_and_shift(tiles)
+                nc.vector.bn_stats(out=stats[:, t, :], in_=acc[t][:])
+                if t >= 1:
+                    tile_deviation(t - 1)
+            tile_deviation(TILES - 1)
+            gains_and_shifts((range(0, TILES - 1), range(TILES - 1, TILES)))
             for t in range(TILES):
                 store_tile(t)

@@ -69,8 +69,8 @@ def tile_memory_sup_pb_k_kernel(tc, query, concat_memory, conv_w, bn_gamma, bn_b
         q_sb = const.tile([P, BATCH, PLANES, PIXELS], BF16)
         sum_sq = const.tile([P, 2, SQUARE_PASSES], F32)
         inv_norm = const.tile([P, BATCH, PIXELS], F32)
-        q_codes = const.tile([P, HALF_PASSES, ROWS], U32, align_bytes=64)
-        q_scales = const.tile([P, HALF_PASSES, ROWS], U8, align_bytes=64)
+        q_codes = const.tile([P, HALF_PASSES, ROWS], U32, align_bytes=256)
+        q_scales = const.tile([P, HALF_PASSES, ROWS], U8, align_bytes=256)
         acc = [acc_pool.tile([P, ROWS], F32, name="acc%d" % t) for t in range(TILES)]
 
         def load_slab(slab):
@@ -216,30 +216,47 @@ def tile_memory_sup_pb_k_kernel(tc, query, concat_memory, conv_w, bn_gamma, bn_b
 
         scales_of = {}
 
-        def pixel_scales_start(b):
-            products = scratch.tile([P, 2, P], F32, tag="products", name="products")
-            nc.vector.tensor_tensor(
-                out=products[:], in0=gram_of[b][:], in1=ident[:].unsqueeze(1).to_broadcast([P, 2, P]), op=ALU.mult
-            )
-            total = scratch.tile([P, 2], F32, tag="total", name="total")
-            nc.vector.tensor_reduce(out=total[:], in_=products[:], axis=AXIS.X, op=ALU.add)
-            if b == 1:
-                squared = scratch.tile([P, 2], F32, tag="squared", name="squared")
-                nc.vector.tensor_reduce(out=squared[:], in_=sum_sq[:], axis=AXIS.X, op=ALU.add)
-                both = scratch.tile([P, 2], F32, tag="both", name="both")
-                nc.vector.tensor_tensor(out=both[:], in0=total[:], in1=squared[:], op=ALU.add)
-                total = both
-                banks["count"] = TRANSPOSE_BANKS
-            floored = scratch.tile([P, 2], F32, tag="floored", name="floored")
-            nc.vector.tensor_scalar_max(out=floored[:], in0=total[:], scalar1=L2_EPS * L2_EPS)
-            norm = scratch.tile([P, 2], F32, tag="norm", name="norm")
-            nc.scalar.sqrt(out=norm[:], in_=floored[:])
-            inv = scratch.tile([P, 2], F32, tag="inv", name="inv")
-            nc.vector.reciprocal(out=inv[:], in_=norm[:])
-            diagonal = scratch.tile([P, 2, P], F32, tag="diagonal", name="diagonal")
-            for h in range(2):
-                nc.vector.tensor_scalar_mul(out=diagonal[:, h, :], in0=ident[:], scalar1=inv[:, h : h + 1])
-            scales_of[b] = diagonal
+        def pixel_scale_steps(b):
+            totals = {}
+
+            def sum_diagonals():
+                if b == 1:
+                    totals["squared"] = scratch.tile([P, 2], F32, tag="squared", name="squared")
+                    nc.vector.tensor_reduce(out=totals["squared"][:], in_=sum_sq[:], axis=AXIS.X, op=ALU.add)
+                    banks["count"] = TRANSPOSE_BANKS
+                products = scratch.tile([P, 2, P], F32, tag="products", name="products")
+                totals["multiplied"] = scratch.tile([P, 2], F32, tag="multiplied", name="multiplied")
+                for h in range(2):
+                    nc.vector.scalar_tensor_tensor(
+                        out=products[:, h, :],
+                        in0=gram_of[b][:, h, :],
+                        scalar=1.0,
+                        in1=ident[:],
+                        op0=ALU.mult,
+                        op1=ALU.mult,
+                        accum_out=totals["multiplied"][:, h : h + 1],
+                    )
+
+            def root():
+                total = totals["multiplied"]
+                if b == 1:
+                    total = scratch.tile([P, 2], F32, tag="total", name="total")
+                    nc.vector.tensor_tensor(
+                        out=total[:], in0=totals["multiplied"][:], in1=totals["squared"][:], op=ALU.add
+                    )
+                floored = scratch.tile([P, 2], F32, tag="floored", name="floored")
+                nc.vector.tensor_scalar_max(out=floored[:], in0=total[:], scalar1=L2_EPS * L2_EPS)
+                totals["norm"] = scratch.tile([P, 2], F32, tag="norm", name="norm")
+                nc.scalar.sqrt(out=totals["norm"][:], in_=floored[:])
+
+            def invert():
+                inv = scratch.tile([P, 2], F32, tag="inv", name="inv")
+                nc.vector.reciprocal(out=inv[:], in_=totals["norm"][:])
+                scales_of[b] = scratch.tile([P, 2, P], F32, tag="diagonal", name="diagonal")
+                for h in range(2):
+                    nc.vector.tensor_scalar_mul(out=scales_of[b][:, h, :], in0=ident[:], scalar1=inv[:, h : h + 1])
+
+            return [sum_diagonals, root, invert]
 
         def pixel_scales_spread(b):
             bank = next_bank()
@@ -251,9 +268,9 @@ def tile_memory_sup_pb_k_kernel(tc, query, concat_memory, conv_w, bn_gamma, bn_b
                 stop=True,
             )
             if b == 0:
-                nc.vector.tensor_copy(out=inv_norm[:, b, :], in_=bank[:, 0:2, :].rearrange("p h r -> p (h r)"))
+                nc.scalar.copy(out=inv_norm[:, b, :], in_=bank[:, 0:2, :].rearrange("p h r -> p (h r)"))
             else:
-                nc.vector.tensor_copy(
+                nc.scalar.copy(
                     out=inv_norm[:, b, :].rearrange("p (r h) -> p r h", h=2),
                     in_=bank[:, 0:2, :].rearrange("p h r -> p r h"),
                 )
@@ -332,8 +349,8 @@ def tile_memory_sup_pb_k_kernel(tc, query, concat_memory, conv_w, bn_gamma, bn_b
 
         def quantise(i):
             width = OUT_CH + (ROWS if passes[i][0] == "memory" else 0)
-            codes = work.tile([P, OUT_CH + ROWS], U32, tag="codes", align_bytes=64)
-            scales = work.tile([P, OUT_CH + ROWS], U8, tag="scales", align_bytes=64)
+            codes = work.tile([P, OUT_CH + ROWS], U32, tag="codes", align_bytes=256)
+            scales = work.tile([P, OUT_CH + ROWS], U8, tag="scales", align_bytes=256)
             nc.vector.quantize_mx(
                 out=codes[:, 0:width].bitcast(FP8X4), scales=scales[:, 0:width], in_=grouped_of[i][:, 0 : 4 * width]
             )
@@ -360,7 +377,7 @@ def tile_memory_sup_pb_k_kernel(tc, query, concat_memory, conv_w, bn_gamma, bn_b
         std = const.tile([P, TILES], F32)
         inv_std = const.tile([P, TILES], F32)
         gain = const.tile([P, TILES], F32)
-        mean_gain = const.tile([P, TILES], F32)
+        minus_gain = const.tile([P, TILES], F32)
         shift = const.tile([P, TILES], F32)
         out_tiles = out.rearrange("b (t p) h w -> t p b (h w)", p=P)
 
@@ -370,25 +387,31 @@ def tile_memory_sup_pb_k_kernel(tc, query, concat_memory, conv_w, bn_gamma, bn_b
             nc.vector.bn_aggr(out=mean_var[:, t, :], in_=stats[:, t, :])
             nc.scalar.activation(out=std[:, t : t + 1], in_=mean_var[:, t, 1:2], func=ACT.Sqrt, bias=BN_EPS)
 
-        def gains_and_shifts(groups):
-            columns = [slice(tiles.start, tiles.stop) for tiles in groups]
-            for cols in columns:
-                nc.vector.reciprocal(out=inv_std[:, cols], in_=std[:, cols])
-            for cols in columns:
-                nc.vector.tensor_tensor(out=gain[:, cols], in0=gamma_beta[:, cols], in1=inv_std[:, cols], op=ALU.mult)
-            for cols in columns:
-                nc.vector.tensor_tensor(out=mean_gain[:, cols], in0=mean_var[:, cols, 0], in1=gain[:, cols], op=ALU.mult)
-            for cols in columns:
-                beta = gamma_beta[:, TILES + cols.start : TILES + cols.stop]
-                nc.vector.tensor_tensor(out=shift[:, cols], in0=beta, in1=mean_gain[:, cols], op=ALU.subtract)
+        def gains_and_shifts():
+            gamma = gamma_beta[:, 0:TILES]
+            nc.vector.reciprocal(out=inv_std[:], in_=std[:])
+            nc.vector.scalar_tensor_tensor(
+                out=minus_gain[:], in0=inv_std[:], scalar=-1.0, in1=gamma, op0=ALU.mult, op1=ALU.mult
+            )
+            nc.vector.tensor_tensor(out=gain[:], in0=gamma, in1=inv_std[:], op=ALU.mult)
+            for t in range(TILES):
+                nc.vector.scalar_tensor_tensor(
+                    out=shift[:, t : t + 1],
+                    in0=mean_var[:, t, 0:1],
+                    scalar=minus_gain[:, t : t + 1],
+                    in1=gamma_beta[:, TILES + t : TILES + t + 1],
+                    op0=ALU.mult,
+                    op1=ALU.add,
+                )
 
-        def store_tile(t):
-            result = const.tile([P, BATCH, PIXELS], F32, name="result%d" % t)
+        def store(t, batches, on_vector):
+            pixels = slice(batches.start * PIXELS, batches.stop * PIXELS)
+            result = const.tile([P, len(batches), PIXELS], F32, name="result%d%d" % (t, batches.start))
             flat = result[:].rearrange("p b n -> p (b n)")
-            if t == 1:
+            if on_vector:
                 nc.vector.tensor_scalar(
                     out=flat,
-                    in0=acc[t][:],
+                    in0=acc[t][:, pixels],
                     scalar1=gain[:, t : t + 1],
                     scalar2=shift[:, t : t + 1],
                     op0=ALU.mult,
@@ -397,9 +420,9 @@ def tile_memory_sup_pb_k_kernel(tc, query, concat_memory, conv_w, bn_gamma, bn_b
                 nc.vector.tensor_scalar_max(out=flat, in0=flat, scalar1=0.0)
             else:
                 nc.scalar.activation(
-                    out=flat, in_=acc[t][:], func=ACT.Relu, scale=gain[:, t : t + 1], bias=shift[:, t : t + 1]
+                    out=flat, in_=acc[t][:, pixels], func=ACT.Relu, scale=gain[:, t : t + 1], bias=shift[:, t : t + 1]
                 )
-            nc.sync.dma_start(out=out_tiles[t], in_=result[:])
+            nc.sync.dma_start(out=out_tiles[t, :, batches.start : batches.stop], in_=result[:])
 
         for c in range(AHEAD):
             load_for_chunk(c)
@@ -415,10 +438,16 @@ def tile_memory_sup_pb_k_kernel(tc, query, concat_memory, conv_w, bn_gamma, bn_b
                     quantise(i - 1)
                 if i == 1:
                     nc.vector.tensor_copy(out=gb_f32[:], in_=gb_rows[:])
+                steps = pixel_scale_steps(scales_due[i + 1]) if i + 1 in scales_due else []
+                for step in steps[:1]:
+                    step()
                 quantise_slices(made)
-                if i + 1 in scales_due:
-                    pixel_scales_start(scales_due[i + 1])
-                made = normalise(slices)
+                for step in steps[1:2]:
+                    step()
+                made = normalise(slices[:1])
+                for step in steps[2:]:
+                    step()
+                made.extend(normalise(slices[1:]))
                 if i < HALF_PASSES:
                     due = [i - LAG] if i >= LAG else []
                 else:
@@ -435,6 +464,9 @@ def tile_memory_sup_pb_k_kernel(tc, query, concat_memory, conv_w, bn_gamma, bn_b
                 if t >= 1:
                     tile_deviation(t - 1)
             tile_deviation(TILES - 1)
-            gains_and_shifts((range(0, TILES - 1), range(TILES - 1, TILES)))
-            for t in range(TILES):
-                store_tile(t)
+            gains_and_shifts()
+            store(0, range(BATCH), False)
+            store(1, range(BATCH), True)
+            store(2, range(BATCH), False)
+            store(3, range(0, 1), False)
+            store(3, range(1, 2), True)

from contextlib import ExitStack

import concourse.mybir as mybir
from concourse.masks import make_identity

F32 = mybir.dt.float32
BF16 = mybir.dt.bfloat16
U32 = mybir.dt.uint32
U8 = mybir.dt.uint8
FP8X4 = mybir.dt.float8_e4m3fn_x4
ACT = mybir.ActivationFunctionType
ALU = mybir.AluOpType
AXIS = mybir.AxisListType

P = 128
BATCH = 2
CHANNELS = 8192
PIXELS = 256
ROWS = BATCH * PIXELS
OUT_CH = 512
TILES = OUT_CH // P
K_PASS = 4 * P
HALF_PASSES = CHANNELS // K_PASS
CHUNK_PASSES = 2
K_CHUNK = CHUNK_PASSES * K_PASS
PLANES = CHANNELS // P
BANK_PLANES = 4
BATCH_BANKS = PLANES // BANK_PLANES
SLAB_PLANES = 8
BATCH_SLABS = PLANES // SLAB_PLANES
FIRST_PASSES = 3
GRAM_SLABS = 2
GRAM_END = FIRST_PASSES + BATCH_SLABS // GRAM_SLABS
SQUARE_PASSES = BATCH_BANKS // 2
SQUARE_END = GRAM_END + SQUARE_PASSES
RUN = 4
TRANSPOSE_BANKS = 4
AHEAD = 2
LAG = 2
L2_EPS = 1e-12
BN_EPS = 1e-5

FLOPS = 2 * ROWS * OUT_CH * 2 * CHANNELS


def tile_memory_sup_pb_k_kernel(tc, query, concat_memory, conv_w, bn_gamma, bn_beta, out):
    nc = tc.nc
    with ExitStack() as ctx:
        const = ctx.enter_context(tc.tile_pool(name="const", bufs=1))
        rows_pool = ctx.enter_context(tc.tile_pool(name="rows", bufs=AHEAD + 1))
        ordered_pool = ctx.enter_context(tc.tile_pool(name="ordered", bufs=2))
        work = ctx.enter_context(tc.tile_pool(name="work", bufs=LAG + 1))
        scratch = ctx.enter_context(tc.tile_pool(name="scratch", bufs=2))
        acc_pool = ctx.enter_context(tc.psum_pool(name="acc", bufs=1))
        bank_pool = ctx.enter_context(tc.psum_pool(name="bank", bufs=1))

        gb_rows = const.tile([P, P], BF16)
        nc.vector.memset(gb_rows[:], 0.0)
        nc.scalar.dma_start(out=gb_rows[0:TILES, :], in_=bn_gamma.rearrange("(t p) -> t p", p=P))
        nc.scalar.dma_start(out=gb_rows[TILES : 2 * TILES, :], in_=bn_beta.rearrange("(t p) -> t p", p=P))
        gamma_beta = const.tile([P, 2 * TILES], F32)
        ones = const.tile([P, P], F32)
        nc.vector.memset(ones[:], 1.0)
        warm = const.tile([P, 1], F32)
        nc.scalar.sqrt(out=warm[:], in_=ones[:, 0:1])
        ident = const.tile([P, P], F32)
        make_identity(nc, ident[:])

        q_sb = const.tile([P, BATCH, PLANES, PIXELS], BF16)
        sum_sq = const.tile([P, 2, SQUARE_PASSES], F32)
        inv_norm = const.tile([P, BATCH, PIXELS], F32)
        q_codes = const.tile([P, HALF_PASSES, ROWS], U32, align_bytes=256)
        q_scales = const.tile([P, HALF_PASSES, ROWS], U8, align_bytes=256)
        acc = [acc_pool.tile([P, ROWS], F32, name="acc%d" % t) for t in range(TILES)]

        def load_slab(slab):
            b, first = divmod(slab * SLAB_PLANES, PLANES)
            nc.sync.dma_start(
                out=q_sb[:, b, first : first + SLAB_PLANES, :].rearrange("p (s e) n -> p s (e n)", e=4),
                in_=query[b, first * P : (first + SLAB_PLANES) * P].rearrange("(s p e) h w -> p s (e h w)", p=P, e=4),
            )

        passes = [("memory", g) for g in range(HALF_PASSES)] + [("query", g) for g in range(HALF_PASSES)]
        chunk_rows = {}

        def load_rows(c, kind, first, count):
            half, g = passes[c * CHUNK_PASSES]
            column = (g + first) * K_PASS
            source = concat_memory
            if kind == "w":
                source = conv_w
                column += CHANNELS if half == "memory" else 0
            if (c, kind) not in chunk_rows:
                chunk_rows[c, kind] = rows_pool.tile([P, TILES, K_CHUNK], BF16, tag="%s_rows" % kind, name="rows")
            parts = 2 if c == 0 and first == 0 and kind == "w" else 1
            size = TILES // parts
            for part in range(parts):
                tiles = slice(size * part, size * (part + 1))
                nc.sync.dma_start(
                    out=chunk_rows[c, kind][:, tiles, first * K_PASS : (first + count) * K_PASS],
                    in_=source[tiles.start * P : tiles.stop * P, column : column + count * K_PASS].rearrange(
                        "(t p) k -> p t k", p=P
                    ),
                )

        banks = {"next": 0, "count": TRANSPOSE_BANKS}

        def next_bank():
            k = banks["next"] % banks["count"]
            banks["next"] = k + 1
            return bank_pool.tile([P, 4, P], F32, tag="bank%d" % k, name="bank%d" % k)

        def slabs_multiplied(i):
            if FIRST_PASSES <= i < GRAM_END:
                return range(GRAM_SLABS * (i - FIRST_PASSES), GRAM_SLABS * (i - FIRST_PASSES + 1))
            return range(0)

        def banks_squared(i):
            if GRAM_END <= i < SQUARE_END:
                return range(BATCH_BANKS // 2 + i - GRAM_END, BATCH_BANKS // 2 + i - GRAM_END + 1)
            return range(0)

        def load_for_chunk(c):
            if c * CHUNK_PASSES >= len(passes):
                return
            step = 1 if c < 2 else CHUNK_PASSES
            for first in range(0, CHUNK_PASSES, step):
                part = range(c * CHUNK_PASSES + first, c * CHUNK_PASSES + first + step)
                slabs = [s for i in part for s in slabs_multiplied(i)]
                for i in part:
                    for k in banks_squared(i):
                        if k % 2 == 0:
                            slabs.extend([BATCH_SLABS + (k - BATCH_BANKS // 2) // 2, BATCH_SLABS + k // 2])
                load_rows(c, "w", first, step)
                for slab in slabs[: len(slabs) // 2]:
                    load_slab(slab)
                if passes[c * CHUNK_PASSES][0] == "memory":
                    load_rows(c, "m", first, step)
                for slab in slabs[len(slabs) // 2 :]:
                    load_slab(slab)

        ordered_of = {}

        def order_engine(i, operand, pair):
            if i == 0 and operand == "w":
                return None
            if i < GRAM_END:
                return nc.vector.tensor_copy
            if i < HALF_PASSES or pair == 1:
                return None
            return nc.scalar.copy

        def order_rows(i):
            if i >= len(passes):
                return
            c, local = divmod(i, CHUNK_PASSES)
            for operand in ("w", "m") if passes[i][0] == "memory" else ("w",):
                for pair in range(TILES // 2):
                    copy = order_engine(i, operand, pair)
                    if copy is None:
                        continue
                    ordered = ordered_pool.tile([P, 2, 2, P], F32, tag="%s%d" % (operand, pair), name="ordered")
                    words = chunk_rows[c, operand][:, 2 * pair : 2 * pair + 2, local * K_PASS : (local + 1) * K_PASS]
                    copy(out=ordered[:], in_=words.bitcast(F32).rearrange("p t (w u) -> p t u w", u=2))
                    ordered_of[i, operand, pair] = ordered

        def transpose_rows(i, operand, pair, grouped_words):
            c, local = divmod(i, CHUNK_PASSES)
            bank = next_bank()
            for j in range(4):
                t, u = divmod(j, 2)
                if (i, operand, pair) in ordered_of:
                    words = ordered_of[i, operand, pair][:, t, u, :]
                else:
                    words = chunk_rows[c, operand][:, 2 * pair + t, :].bitcast(F32)
                    words = words[:, 2 * P * local + u : 2 * P * (local + 1) : 2]
                nc.tensor.transpose(bank[:, j, :], words, ident[:])
            nc.scalar.copy(
                out=grouped_words[:, 4 * P * pair : 4 * P * (pair + 1)].rearrange("p (t r u) -> p t r u", t=2, u=2),
                in_=bank[:].rearrange("p (t u) r -> p t r u", u=2),
            )

        def square_bank(k):
            bank = next_bank()
            for j in range(BANK_PLANES):
                nc.tensor.transpose(bank[:, j, :], q_sb[:, 1, k * BANK_PLANES + j, :].bitcast(F32), ident[:])
            by_parity = bank[:].bitcast(BF16).rearrange("p j (c h) -> p h j c", h=2)
            for h in range(2):
                squares = scratch.tile([P, 4, P], BF16, tag="squares")
                nc.scalar.activation(
                    out=squares[:],
                    in_=by_parity[:, h],
                    func=ACT.Square,
                    accum_out=sum_sq[:, h, k - BATCH_BANKS // 2 : k - BATCH_BANKS // 2 + 1],
                )

        gram_of = {}

        def multiply_planes(b, planes, count):
            if b not in gram_of:
                banks["count"] = TRANSPOSE_BANKS - 1
                gram_of[b] = bank_pool.tile([P, 2, P], F32, tag="bank%d" % (TRANSPOSE_BANKS - 1), name="gram")
            for plane in planes:
                for h in range(2):
                    pixels = q_sb[:, b, plane, h * P : (h + 1) * P] if b == 0 else q_sb[:, b, plane, h::2]
                    nc.tensor.matmul(
                        gram_of[b][:, h, :],
                        lhsT=pixels,
                        rhs=pixels,
                        start=(plane == 0 and h == 0),
                        stop=(plane == count - 1 and h == 1),
                    )

        def multiply_slab(slab):
            multiply_planes(0, range(slab * SLAB_PLANES, (slab + 1) * SLAB_PLANES), PLANES)

        scales_of = {}

        def pixel_scale_steps(b):
            totals = {}

            def sum_diagonals():
                if b == 1:
                    totals["squared"] = scratch.tile([P, 2], F32, tag="squared", name="squared")
                    nc.vector.tensor_reduce(out=totals["squared"][:], in_=sum_sq[:], axis=AXIS.X, op=ALU.add)
                    banks["count"] = TRANSPOSE_BANKS
                products = scratch.tile([P, 2, P], F32, tag="products", name="products")
                totals["multiplied"] = scratch.tile([P, 2], F32, tag="multiplied", name="multiplied")
                for h in range(2):
                    nc.vector.scalar_tensor_tensor(
                        out=products[:, h, :],
                        in0=gram_of[b][:, h, :],
                        scalar=1.0,
                        in1=ident[:],
                        op0=ALU.mult,
                        op1=ALU.mult,
                        accum_out=totals["multiplied"][:, h : h + 1],
                    )

            def root():
                total = totals["multiplied"]
                if b == 1:
                    total = scratch.tile([P, 2], F32, tag="total", name="total")
                    nc.vector.tensor_tensor(
                        out=total[:], in0=totals["multiplied"][:], in1=totals["squared"][:], op=ALU.add
                    )
                floored = scratch.tile([P, 2], F32, tag="floored", name="floored")
                nc.vector.tensor_scalar_max(out=floored[:], in0=total[:], scalar1=L2_EPS * L2_EPS)
                totals["norm"] = scratch.tile([P, 2], F32, tag="norm", name="norm")
                nc.scalar.sqrt(out=totals["norm"][:], in_=floored[:])

            def invert():
                inv = scratch.tile([P, 2], F32, tag="inv", name="inv")
                nc.vector.reciprocal(out=inv[:], in_=totals["norm"][:])
                scales_of[b] = scratch.tile([P, 2, P], F32, tag="diagonal", name="diagonal")
                for h in range(2):
                    nc.vector.tensor_scalar_mul(out=scales_of[b][:, h, :], in0=ident[:], scalar1=inv[:, h : h + 1])

            return [sum_diagonals, root, invert]

        def pixel_scales_spread(b):
            bank = next_bank()
            nc.tensor.matmul(
                bank[:, 0:2, :].rearrange("p h r -> p (h r)"),
                lhsT=ones[:],
                rhs=scales_of[b][:].rearrange("p h r -> p (h r)"),
                start=True,
                stop=True,
            )
            if b == 0:
                nc.scalar.copy(out=inv_norm[:, b, :], in_=bank[:, 0:2, :].rearrange("p h r -> p (h r)"))
            else:
                nc.scalar.copy(
                    out=inv_norm[:, b, :].rearrange("p (r h) -> p r h", h=2),
                    in_=bank[:, 0:2, :].rearrange("p h r -> p r h"),
                )

        gb_f32 = const.tile([P, P], F32)

        def transpose_gamma_beta():
            bank = next_bank()
            nc.tensor.transpose(bank[:, 0, :], gb_f32[:], ident[:])
            nc.vector.tensor_copy(out=gamma_beta[:], in_=bank[:, 0, 0 : 2 * TILES])

        slices_left = [(b, g) for b in range(BATCH) for g in range(HALF_PASSES)]

        def normalise(slices):
            made = []
            for b, g in slices:
                q_flat = work.tile([P, PIXELS, 4], BF16, tag="q_flat", align_bytes=64)
                nc.vector.tensor_tensor(
                    out=q_flat[:].rearrange("p (c i) t -> p c t i", i=RUN),
                    in0=q_sb[:, b, 4 * g : 4 * g + 4, :].rearrange("p t (c i) -> p c t i", i=RUN),
                    in1=inv_norm[:, b, :]
                    .rearrange("p (c i) -> p c i", i=RUN)
                    .unsqueeze(2)
                    .to_broadcast([P, PIXELS // RUN, 4, RUN]),
                    op=ALU.mult,
                )
                made.append((b, g, q_flat[:].rearrange("p n t -> p (n t)")))
            return made

        def quantise_slices(slices):
            for b, g, q_flat in slices:
                pixels = slice(b * PIXELS, (b + 1) * PIXELS)
                nc.vector.quantize_mx(out=q_codes[:, g, pixels].bitcast(FP8X4), scales=q_scales[:, g, pixels], in_=q_flat)

        scales_due = {GRAM_END: 0, SQUARE_END: 1}
        grouped_of = {}
        operands_of = {}

        def prepare(i):
            kind, g = passes[i]
            c, local = divmod(i, CHUNK_PASSES)
            if local == 0:
                load_for_chunk(c + AHEAD)
            grouped = work.tile([P, 4 * (OUT_CH + ROWS)], BF16, tag="grouped", align_bytes=64)
            words = grouped[:].bitcast(F32)
            to_copy = [("w", pair, words[:, 0 : 2 * OUT_CH]) for pair in range(TILES // 2)]
            if kind == "memory":
                to_copy.extend([("m", pair, words[:, 2 * OUT_CH : 2 * (OUT_CH + ROWS)]) for pair in range(TILES // 2)])
            to_multiply = list(slabs_multiplied(i))
            to_square = list(banks_squared(i))
            for k in range(len(to_copy)):
                if k < len(to_square):
                    square_bank(to_square[k])
                operand, pair, half = to_copy[k]
                transpose_rows(i, operand, pair, half)
                if k == 0 and i in scales_due:
                    pixel_scales_spread(scales_due[i])
                    if i == SQUARE_END:
                        transpose_gamma_beta()
                if pair == TILES // 2 - 1:
                    for slab in to_multiply[:1] if operand == "w" else to_multiply[1:]:
                        multiply_slab(slab)
                    if operand == "w" and GRAM_END <= i < SQUARE_END:
                        first = BANK_PLANES * (i - GRAM_END)
                        multiply_planes(1, range(first, first + BANK_PLANES), PLANES // 2)
            grouped_of[i] = grouped
            if i < GRAM_END:
                count = 0
            elif i <= SQUARE_END:
                count = 2
            else:
                count = 1
            slices = slices_left[:count]
            slices_left[:] = slices_left[count:]
            return slices

        def quantise(i):
            width = OUT_CH + (ROWS if passes[i][0] == "memory" else 0)
            codes = work.tile([P, OUT_CH + ROWS], U32, tag="codes", align_bytes=256)
            scales = work.tile([P, OUT_CH + ROWS], U8, tag="scales", align_bytes=256)
            nc.vector.quantize_mx(
                out=codes[:, 0:width].bitcast(FP8X4), scales=scales[:, 0:width], in_=grouped_of[i][:, 0 : 4 * width]
            )
            operands_of[i] = (codes, scales)

        def multiply(i, t):
            kind, g = passes[i]
            codes, scales = operands_of[i]
            if kind == "memory":
                upd_codes, upd_scales = codes[:, OUT_CH : OUT_CH + ROWS], scales[:, OUT_CH : OUT_CH + ROWS]
            else:
                upd_codes, upd_scales = q_codes[:, g, :], q_scales[:, g, :]
            nc.tensor.matmul_mx(
                out=acc[t][:],
                lhsT=codes[:, t * P : (t + 1) * P].bitcast(FP8X4),
                lhsT_scale=scales[:, t * P : (t + 1) * P],
                rhs=upd_codes.bitcast(FP8X4),
                rhs_scale=upd_scales,
                start=(i == 0),
                stop=(i == len(passes) - 1),
            )

        mean_var = const.tile([P, TILES, 2], F32)
        std = const.tile([P, TILES], F32)
        inv_std = const.tile([P, TILES], F32)
        gain = const.tile([P, TILES], F32)
        minus_gain = const.tile([P, TILES], F32)
        shift = const.tile([P, TILES], F32)
        out_tiles = out.rearrange("b (t p) h w -> t p b (h w)", p=P)

        stats = const.tile([P, TILES, 6], F32)

        def tile_deviation(t):
            nc.vector.bn_aggr(out=mean_var[:, t, :], in_=stats[:, t, :])
            nc.scalar.activation(out=std[:, t : t + 1], in_=mean_var[:, t, 1:2], func=ACT.Sqrt, bias=BN_EPS)

        def gains_and_shifts():
            gamma = gamma_beta[:, 0:TILES]
            nc.vector.reciprocal(out=inv_std[:], in_=std[:])
            nc.vector.scalar_tensor_tensor(
                out=minus_gain[:], in0=inv_std[:], scalar=-1.0, in1=gamma, op0=ALU.mult, op1=ALU.mult
            )
            nc.vector.tensor_tensor(out=gain[:], in0=gamma, in1=inv_std[:], op=ALU.mult)
            for t in range(TILES):
                nc.vector.scalar_tensor_tensor(
                    out=shift[:, t : t + 1],
                    in0=mean_var[:, t, 0:1],
                    scalar=minus_gain[:, t : t + 1],
                    in1=gamma_beta[:, TILES + t : TILES + t + 1],
                    op0=ALU.mult,
                    op1=ALU.add,
                )

        def store(t, batches, on_vector):
            pixels = slice(batches.start * PIXELS, batches.stop * PIXELS)
            result = const.tile([P, len(batches), PIXELS], F32, name="result%d%d" % (t, batches.start))
            flat = result[:].rearrange("p b n -> p (b n)")
            if on_vector:
                nc.vector.tensor_scalar(
                    out=flat,
                    in0=acc[t][:, pixels],
                    scalar1=gain[:, t : t + 1],
                    scalar2=shift[:, t : t + 1],
                    op0=ALU.mult,
                    op1=ALU.add,
                )
                nc.vector.tensor_scalar_max(out=flat, in0=flat, scalar1=0.0)
            else:
                nc.scalar.activation(
                    out=flat, in_=acc[t][:, pixels], func=ACT.Relu, scale=gain[:, t : t + 1], bias=shift[:, t : t + 1]
                )
            nc.sync.dma_start(out=out_tiles[t, :, batches.start : batches.stop], in_=result[:])

        for c in range(AHEAD):
            load_for_chunk(c)

        with tc.manual_schedule():
            order_rows(0)
            made = []
            for i in range(len(passes)):
                if i + 1 < len(passes):
                    order_rows(i + 1)
                slices = prepare(i)
                if i >= 1:
                    quantise(i - 1)
                if i == 1:
                    nc.vector.tensor_copy(out=gb_f32[:], in_=gb_rows[:])
                steps = pixel_scale_steps(scales_due[i + 1]) if i + 1 in scales_due else []
                for step in steps[:1]:
                    step()
                quantise_slices(made)
                for step in steps[1:2]:
                    step()
                made = normalise(slices[:1])
                for step in steps[2:]:
                    step()
                made.extend(normalise(slices[1:]))
                if i < HALF_PASSES:
                    due = [i - LAG] if i >= LAG else []
                else:
                    due = [i - LAG - 1, i - LAG] if i % 2 == 1 else []
                for k in due:
                    for t in range(TILES):
                        multiply(k, t)
            quantise_slices(made)
            quantise(len(passes) - 1)
            for t in range(TILES):
                for i in range(len(passes) - LAG, len(passes)):
                    multiply(i, t)
                nc.vector.bn_stats(out=stats[:, t, :], in_=acc[t][:])
                if t >= 1:
                    tile_deviation(t - 1)
            tile_deviation(TILES - 1)
            gains_and_shifts()
            store(0, range(BATCH), False)
            store(1, range(BATCH), True)
            store(2, range(BATCH), False)
            store(3, range(0, 1), False)
            store(3, range(1, 2), True)
